import numpy as np
import ml_dtypes


def mxq(x, axis, fmt="e4m3"):
    dtype, down = {"e4m3": (ml_dtypes.float8_e4m3fn, 7), "e5m2": (ml_dtypes.float8_e5m2, 14)}[fmt]
    v = np.moveaxis(np.asarray(x, np.float32).astype(ml_dtypes.bfloat16).astype(np.float64), axis, -1)
    blocks = v.reshape(v.shape[:-1] + (-1, 32))
    amax = np.abs(blocks).max(-1, keepdims=True)
    byte = np.maximum(np.where(amax > 0, np.frexp(amax)[1] - 1 + 127, 0) - down, 1)
    scale = np.exp2(byte - 127.0)
    codes = (blocks / scale).astype(np.float32).astype(dtype).astype(np.float64)
    return np.moveaxis((codes * scale).reshape(v.shape), -1, axis)


WIDE = False


def mx_kscale(k):
    if not WIDE:
        return np.ones(k)
    levels = np.array([10, -10, 5, -5, 0])
    a = np.random.permutation(np.resize(levels, k // 512 * 4)).reshape(k // 512, 4)
    idx = np.arange(k)
    return np.exp2(a[idx // 512, idx % 128 // 32])


BF16 = ml_dtypes.bfloat16


def bf(x):
    return np.asarray(x, np.float32).astype(BF16)


def f64(x):
    return np.asarray(x).astype(np.float64)


N, N_CH, D, H = 4096, 8, 8, 128


def sigmoid(v):
    return 1.0 / (1.0 + np.exp(-v))


def setup_inputs():
    s = mx_kscale(D * H).reshape(D, H)
    return {
        "neighbour_h": bf(np.random.standard_normal((N, N_CH, H)) * s[:N_CH]),
        "neighbour_c": bf(np.random.standard_normal((N, N_CH, H))),
        "f_input": bf(np.random.standard_normal((N, H))),
        "iou_input": bf(np.random.standard_normal((N, 3 * H)) * 0.5),
        "U_f": bf(np.random.standard_normal((D, H, H)) * 0.8 / np.sqrt(H) / s[:, None, :]),
        "U_iou": bf(np.random.standard_normal((D, 3 * H, H)) * 1.6 / np.sqrt(D * H) / s[:, None, :]),
    }


def reference(neighbour_h, neighbour_c, f_input, iou_input, U_f, U_iou):
    n, n_ch, h = neighbour_h.shape
    d = U_f.shape[0]
    pad = d - n_ch
    nh = np.pad(f64(neighbour_h), ((0, 0), (0, pad), (0, 0)))
    ncl = np.pad(f64(neighbour_c), ((0, 0), (0, pad), (0, 0)))
    f_logits = (nh.transpose(1, 0, 2) @ f64(U_f).transpose(0, 2, 1)).transpose(1, 0, 2) + f64(f_input)[:, None, :]
    w_iou = f64(U_iou).transpose(0, 2, 1).reshape(d * h, 3 * h)
    iou_aggr = (mxq(nh.reshape(n, d * h), 1, "e4m3") @ mxq(w_iou, 0, "e4m3")) + f64(iou_input)
    f = sigmoid(f_logits)
    c_aggr = np.sum(f * ncl, axis=1)
    iou = f64(iou_input) + iou_aggr
    i, o, u = np.split(iou, 3, axis=1)
    c = sigmoid(i) * np.tanh(u) + c_aggr
    h_out = sigmoid(o) * np.tanh(c)
    return (h_out, c)

@@ -1,0 +1,265 @@
+from contextlib import ExitStack
+
+import concourse.mybir as mybir
+from concourse.masks import make_identity
+
+F32 = mybir.dt.float32
+BF16 = mybir.dt.bfloat16
+U32 = mybir.dt.uint32
+U8 = mybir.dt.uint8
+FP8X4 = mybir.dt.float8_e4m3fn_x4
+ALU = mybir.AluOpType
+ACT = mybir.ActivationFunctionType
+AX = mybir.AxisListType
+
+P = 128
+N_NODES = 4096
+D = 8
+H = 128
+NT = N_NODES // P
+CH = 4
+NCH = NT // CH
+
+FLOPS = 2 * N_NODES * D * H * 3 * H + 2 * N_NODES * D * H * H
+
+
+def tile_generictreelstmcell_t_kernel(
+    tc, neighbour_h, neighbour_c, f_input, iou_input, U_f, U_iou, out_0, out_1
+):
+    nc = tc.nc
+    nh_v = neighbour_h.rearrange("(p t) d h -> p t (d h)", t=NT)
+    c_v = neighbour_c.rearrange("(p t) d h -> p t (d h)", t=NT)
+    b_v = f_input.rearrange("(p t) o -> p t o", t=NT)
+    iou_v = iou_input.rearrange("(p t) j -> p t j", t=NT)
+    h_out_v = out_0.rearrange("(p t) o -> p t o", t=NT)
+    c_out_v = out_1.rearrange("(p t) o -> p t o", t=NT)
+
+    with ExitStack() as ctx:
+        const = ctx.enter_context(tc.tile_pool(name="const", bufs=1))
+        nh_pool = ctx.enter_context(tc.tile_pool(name="nh", bufs=3))
+        c_pool = ctx.enter_context(tc.tile_pool(name="cin", bufs=3))
+        xt_pool = ctx.enter_context(tc.tile_pool(name="xts", bufs=3))
+        q_pool = ctx.enter_context(tc.tile_pool(name="quant", bufs=2))
+        z_pool = ctx.enter_context(tc.tile_pool(name="zb", bufs=6))
+        fin = ctx.enter_context(tc.tile_pool(name="fin", bufs=2))
+        psum = ctx.enter_context(tc.psum_pool(name="psum", bufs=1))
+
+        ufs = const.tile([P, D, H], BF16)
+        nc.sync.dma_start(out=ufs[:], in_=U_f.rearrange("d o h -> o d h"))
+        uis = const.tile([P, 3, D * H], BF16)
+        for jb in range(3):
+            nc.sync.dma_start(
+                out=uis[:, jb, :].rearrange("p (d h) -> p d h", d=D),
+                in_=U_iou[:, jb * P : (jb + 1) * P, :].rearrange("d j h -> j d h"),
+            )
+
+        nh_tiles = {}
+        c_tiles = {}
+
+        def load_nh(c):
+            nh_sb = nh_pool.tile([P, CH, D * H], BF16, name="nh_sb")
+            nc.sync.dma_start(out=nh_sb[:], in_=nh_v[:, c * CH : (c + 1) * CH, :])
+            nh_tiles[c] = nh_sb
+
+        def load_c(c):
+            c_in = c_pool.tile([P, CH, D * H], BF16, name="c_in")
+            nc.sync.dma_start(out=c_in[:], in_=c_v[:, c * CH : (c + 1) * CH, :])
+            c_tiles[c] = c_in
+
+        load_nh(0)
+        b_all = const.tile([P, NT, H], BF16)
+        nc.sync.dma_start(out=b_all[:], in_=b_v)
+        load_c(0)
+        iou_all = const.tile([P, NT, 3 * H], BF16)
+        for q in range(4):
+            nc.sync.dma_start(
+                out=iou_all[:, q * 8 : (q + 1) * 8, :], in_=iou_v[:, q * 8 : (q + 1) * 8, :]
+            )
+            if q == 0:
+                load_nh(1)
+
+        ident_b = const.tile([P, P], BF16)
+        make_identity(nc, ident_b[:])
+        ident_f = const.tile([P, P], F32)
+        make_identity(nc, ident_f[:])
+
+        uf_ps = psum.tile([P, D, H], BF16, tag="xt", bufs=2)
+        for d in range(D):
+            nc.tensor.transpose(uf_ps[:, d, :], ufs[:, d, :], ident_b[:])
+        ufT = const.tile([P, D, H], BF16)
+        nc.vector.tensor_copy(out=ufT[:], in_=uf_ps[:])
+
+        wg = const.tile([P, 2, 3 * H, 2], F32, align_bytes=64)
+        for g in range(2):
+            for jb in range(3):
+                w_ps = psum.tile([P, 2, P], F32, tag="wt", bufs=1)
+                for u in range(2):
+                    s = 2 * g + u
+                    nc.tensor.transpose(
+                        w_ps[:, u, :],
+                        uis[:, jb, :].bitcast(F32)[:, s * P : (s + 1) * P],
+                        ident_f[:],
+                    )
+                nc.vector.tensor_copy(
+                    out=wg[:, g, jb * P : (jb + 1) * P, :],
+                    in_=w_ps[:].rearrange("p u j -> p j u"),
+                )
+        wcodes = const.tile([P, 2, 3 * H], U32, align_bytes=64)
+        wscales = const.tile([P, 2, 3 * H], U8, align_bytes=64)
+        COLS = ((0, 256), (256, 384))
+        for g in range(2):
+            for j0, j1 in COLS:
+                nc.vector.quantize_mx(
+                    out=wcodes[:, g, j0:j1].bitcast(FP8X4),
+                    scales=wscales[:, g, j0:j1],
+                    in_=wg[:, g, j0:j1, :].rearrange("p j u -> p (j u)").bitcast(BF16),
+                )
+
+        xT_tiles = {}
+        gq_tiles = {}
+        code_tiles = {}
+        ca_tiles = {}
+        iou_tiles = {}
+
+        def transposes_bf16(t):
+            c, tt = divmod(t, CH)
+            xt = psum.tile([P, D, P], BF16, tag="xt", bufs=2)
+            for d in range(D):
+                nc.tensor.transpose(
+                    xt[:, d, :], nh_tiles[c][:, tt, d * H : (d + 1) * H], ident_b[:]
+                )
+            xT = xt_pool.tile([P, D, P], BF16, name="xT")
+            nc.scalar.copy(out=xT[:], in_=xt[:])
+            xT_tiles[t] = xT
+
+        def transposes_words(t):
+            c, tt = divmod(t, CH)
+            if tt == 0:
+                gq_tiles[c] = q_pool.tile([P, CH * 512], F32, name="gq", align_bytes=64)
+            wt = psum.tile([P, 4, P], F32, tag="wt", bufs=1)
+            words = nh_tiles[c][:, tt, :].bitcast(F32)
+            for s in range(4):
+                nc.tensor.transpose(wt[:, s, :], words[:, s * P : (s + 1) * P], ident_f[:])
+            nc.scalar.copy(
+                out=gq_tiles[c][:, tt * 512 : (tt + 1) * 512].rearrange(
+                    "p (g n u) -> p g n u", g=2, u=2
+                ),
+                in_=wt[:].rearrange("p (g u) n -> p g n u", u=2),
+            )
+
+        def quantise(c):
+            codes = q_pool.tile([P, CH * 256], U32, name="codes", align_bytes=64)
+            scales = q_pool.tile([P, CH * 256], U8, name="scales", align_bytes=64)
+            nc.vector.quantize_mx(
+                out=codes[:].bitcast(FP8X4), scales=scales[:], in_=gq_tiles[c][:].bitcast(BF16)
+            )
+            code_tiles[c] = (codes, scales)
+
+        def forget(t):
+            c, tt = divmod(t, CH)
+            if tt == 0:
+                ca_tiles[c] = fin.tile([P, CH, H], F32, name="ca")
+            xT = xT_tiles[t]
+            zb = z_pool.tile([P, 2, H, 4], F32, name="zb")
+            for k in range(2):
+                z = psum.tile([P, 4, H], F32, tag="z", bufs=4)
+                for j in range(4):
+                    d = 4 * k + j
+                    nc.tensor.matmul(
+                        z[:, j, :], lhsT=xT[:, d, :], rhs=ufT[:, d, :], start=True, stop=True
+                    )
+                nc.vector.tensor_tensor(
+                    out=zb[:, k, :, :],
+                    in0=z[:].rearrange("p j o -> p o j"),
+                    in1=b_all[:, t, :].unsqueeze(2).to_broadcast([P, H, 4]),
+                    op=ALU.add,
+                )
+            nc.scalar.activation(out=zb[:], in_=zb[:], func=ACT.Sigmoid)
+            for k in range(2):
+                nc.gpsimd.tensor_tensor(
+                    out=zb[:, k, :, :],
+                    in0=zb[:, k, :, :],
+                    in1=c_tiles[c][:, tt, k * 512 : (k + 1) * 512].rearrange(
+                        "p (j o) -> p o j", j=4
+                    ),
+                    op=ALU.mult,
+                )
+            nc.vector.tensor_reduce(
+                out=ca_tiles[c][:, tt, :],
+                in_=zb[:].rearrange("p k o j -> p o k j"),
+                axis=AX.XY,
+                op=ALU.add,
+            )
+
+        def iou_gate(t):
+            c, tt = divmod(t, CH)
+            if tt == 0:
+                iou_tiles[c] = fin.tile([P, CH, 3 * H], F32, name="iou_sb")
+            codes, scales = code_tiles[c]
+            acc = psum.tile([P, 3 * H], F32, tag="iou", bufs=1)
+            for j0, j1 in COLS:
+                for g in range(2):
+                    n0 = tt * 256 + g * P
+                    nc.tensor.matmul_mx(
+                        out=acc[:, j0:j1],
+                        lhsT=codes[:, n0 : n0 + P].bitcast(FP8X4),
+                        lhsT_scale=scales[:, n0 : n0 + P],
+                        rhs=wcodes[:, g, j0:j1].bitcast(FP8X4),
+                        rhs_scale=wscales[:, g, j0:j1],
+                        start=(g == 0),
+                        stop=(g == 1),
+                    )
+            nc.vector.scalar_tensor_tensor(
+                out=iou_tiles[c][:, tt, :],
+                in0=iou_all[:, t, :],
+                scalar=2.0,
+                in1=acc[:],
+                op0=ALU.mult,
+                op1=ALU.add,
+            )
+
+        def final(c):
+            iou_sb = iou_tiles[c]
+            ts = slice(c * CH, (c + 1) * CH)
+            nc.scalar.activation(
+                out=iou_sb[:, :, 0 : 2 * H], in_=iou_sb[:, :, 0 : 2 * H], func=ACT.Sigmoid
+            )
+            nc.scalar.activation(
+                out=iou_sb[:, :, 2 * H : 3 * H], in_=iou_sb[:, :, 2 * H : 3 * H], func=ACT.Tanh
+            )
+            iu = fin.tile([P, CH, H], F32, name="iu")
+            nc.gpsimd.tensor_tensor(
+                out=iu[:], in0=iou_sb[:, :, 0:H], in1=iou_sb[:, :, 2 * H : 3 * H], op=ALU.mult
+            )
+            c_sb = fin.tile([P, CH, H], F32, name="c_sb")
+            nc.gpsimd.tensor_tensor(out=c_sb[:], in0=iu[:], in1=ca_tiles[c][:], op=ALU.add)
+            nc.sync.dma_start(out=c_out_v[:, ts, :], in_=c_sb[:])
+            tch = fin.tile([P, CH, H], F32, name="tch")
+            nc.scalar.activation(out=tch[:], in_=c_sb[:], func=ACT.Tanh)
+            h_sb = fin.tile([P, CH, H], F32, name="h_sb")
+            nc.gpsimd.tensor_tensor(
+                out=h_sb[:], in0=iou_sb[:, :, H : 2 * H], in1=tch[:], op=ALU.mult
+            )
+            nc.sync.dma_start(out=h_out_v[:, ts, :], in_=h_sb[:])
+
+        transposes_bf16(0)
+        for t in range(CH):
+            transposes_words(t)
+        quantise(0)
+        for t in range(NT):
+            c, tt = divmod(t, CH)
+            if tt == 0:
+                if c + 2 < NCH:
+                    load_nh(c + 2)
+                if c + 1 < NCH:
+                    load_c(c + 1)
+            if t + 1 < NT:
+                transposes_bf16(t + 1)
+            if t + CH < NT:
+                transposes_words(t + CH)
+            forget(t)
+            iou_gate(t)
+            if tt == CH - 1:
+                if c + 1 < NCH:
+                    quantise(c + 1)
+                final(c)

@@ -19,8 +19,18 @@ H = 128
 NT = N_NODES // P
 CH = 4
 NCH = NT // CH
+RHO0 = 6
+COLS = ((0, 256), (256, 384))
 
 FLOPS = 2 * N_NODES * D * H * 3 * H + 2 * N_NODES * D * H * H
+
+
+def rho(t):
+    return max(t, RHO0 + t // 2)
+
+
+def fin_base(c):
+    return max(CH * c + CH, rho(CH * c + CH - 1) + 1)
 
 
 def tile_generictreelstmcell_t_kernel(
@@ -34,232 +44,347 @@ def tile_generictreelstmcell_t_kernel(
     h_out_v = out_0.rearrange("(p t) o -> p t o", t=NT)
     c_out_v = out_1.rearrange("(p t) o -> p t o", t=NT)
 
+    st_rounds = {}
+    for t in range(NT):
+        st_rounds[rho(t)] = st_rounds.get(rho(t), []) + [t]
+
     with ExitStack() as ctx:
         const = ctx.enter_context(tc.tile_pool(name="const", bufs=1))
         nh_pool = ctx.enter_context(tc.tile_pool(name="nh", bufs=3))
         c_pool = ctx.enter_context(tc.tile_pool(name="cin", bufs=3))
         xt_pool = ctx.enter_context(tc.tile_pool(name="xts", bufs=3))
-        q_pool = ctx.enter_context(tc.tile_pool(name="quant", bufs=2))
-        z_pool = ctx.enter_context(tc.tile_pool(name="zb", bufs=6))
+        g_pool = ctx.enter_context(tc.tile_pool(name="grp", bufs=3))
+        q_pool = ctx.enter_context(tc.tile_pool(name="quant", bufs=10))
+        z_pool = ctx.enter_context(tc.tile_pool(name="zb", bufs=4))
+        fin3 = ctx.enter_context(tc.tile_pool(name="fin3", bufs=3))
         fin = ctx.enter_context(tc.tile_pool(name="fin", bufs=2))
         psum = ctx.enter_context(tc.psum_pool(name="psum", bufs=1))
-
-        ufs = const.tile([P, D, H], BF16)
-        nc.sync.dma_start(out=ufs[:], in_=U_f.rearrange("d o h -> o d h"))
-        uis = const.tile([P, 3, D * H], BF16)
-        for jb in range(3):
-            nc.sync.dma_start(
-                out=uis[:, jb, :].rearrange("p (d h) -> p d h", d=D),
-                in_=U_iou[:, jb * P : (jb + 1) * P, :].rearrange("d j h -> j d h"),
-            )
+        ctx.enter_context(tc.manual_schedule())
 
         nh_tiles = {}
         c_tiles = {}
+        xt_ps = {}
+        xT_sb = {}
+        wt_ps = {}
+        gq_sb = {}
+        code_sb = {}
+        z_ps = {}
+        zb_sb = {}
+        acc_ps = {}
+        ca_sb = {}
+        iou_sb = {}
+        iu_sb = {}
+        c_sb = {}
+        tch_sb = {}
+        h_sb = {}
+        wf_ps = {}
 
-        def load_nh(c):
-            nh_sb = nh_pool.tile([P, CH, D * H], BF16, name="nh_sb")
-            nc.sync.dma_start(out=nh_sb[:], in_=nh_v[:, c * CH : (c + 1) * CH, :])
-            nh_tiles[c] = nh_sb
+        def alloc_nh(c):
+            nh_tiles[c] = nh_pool.tile([P, CH, D * H], BF16, name="nh_sb")
 
-        def load_c(c):
-            c_in = c_pool.tile([P, CH, D * H], BF16, name="c_in")
-            nc.sync.dma_start(out=c_in[:], in_=c_v[:, c * CH : (c + 1) * CH, :])
-            c_tiles[c] = c_in
-
-        load_nh(0)
-        b_all = const.tile([P, NT, H], BF16)
-        nc.sync.dma_start(out=b_all[:], in_=b_v)
-        load_c(0)
-        iou_all = const.tile([P, NT, 3 * H], BF16)
-        for q in range(4):
+        def load_nh(c, t0, t1):
             nc.sync.dma_start(
-                out=iou_all[:, q * 8 : (q + 1) * 8, :], in_=iou_v[:, q * 8 : (q + 1) * 8, :]
+                out=nh_tiles[c][:, t0:t1, :], in_=nh_v[:, c * CH + t0 : c * CH + t1, :]
             )
-            if q == 0:
-                load_nh(1)
 
+        def alloc_c(c):
+            c_tiles[c] = c_pool.tile([P, CH, D * H], BF16, name="c_in")
+
+        def load_c(c, t0, t1):
+            nc.sync.dma_start(
+                out=c_tiles[c][:, t0:t1, :], in_=c_v[:, c * CH + t0 : c * CH + t1, :]
+            )
+
+        warm = const.tile([P, 1], F32)
+        nc.vector.memset(warm[:], 0.0)
+        nc.scalar.activation(out=warm[:], in_=warm[:], func=ACT.Sigmoid)
         ident_b = const.tile([P, P], BF16)
         make_identity(nc, ident_b[:])
         ident_f = const.tile([P, P], F32)
         make_identity(nc, ident_f[:])
 
-        uf_ps = psum.tile([P, D, H], BF16, tag="xt", bufs=2)
-        for d in range(D):
-            nc.tensor.transpose(uf_ps[:, d, :], ufs[:, d, :], ident_b[:])
-        ufT = const.tile([P, D, H], BF16)
-        nc.vector.tensor_copy(out=ufT[:], in_=uf_ps[:])
+        ufs = const.tile([P, D, H], BF16)
+        uis = const.tile([P, 3, D * H], BF16)
+        b_all = const.tile([P, NT, H], BF16)
+        iou_all = const.tile([P, NT, 3 * H], BF16)
+        alloc_nh(0)
+        load_nh(0, 0, 1)
+        nc.sync.dma_start(out=ufs[:], in_=U_f.rearrange("d o h -> o d h"))
+        nc.sync.dma_start(out=b_all[:, 0:CH, :], in_=b_v[:, 0:CH, :])
+        load_nh(0, 1, CH)
+        alloc_c(0)
+        load_c(0, 0, 1)
+        alloc_nh(1)
+        load_nh(1, 0, CH)
+        load_c(0, 1, CH)
+        for jb in range(3):
+            nc.sync.dma_start(
+                out=uis[:, jb, :].rearrange("p (d h) -> p d h", d=D),
+                in_=U_iou[:, jb * P : (jb + 1) * P, :].rearrange("d j h -> j d h"),
+            )
+        nc.sync.dma_start(out=iou_all[:, 0:8, :], in_=iou_v[:, 0:8, :])
+        nc.sync.dma_start(out=b_all[:, CH:NT, :], in_=b_v[:, CH:NT, :])
+        alloc_c(1)
+        load_c(1, 0, CH)
+        alloc_nh(2)
+        load_nh(2, 0, CH)
+        nc.sync.dma_start(out=iou_all[:, 8:NT, :], in_=iou_v[:, 8:NT, :])
 
-        wg = const.tile([P, 2, 3 * H, 2], F32, align_bytes=64)
-        for g in range(2):
-            for jb in range(3):
-                w_ps = psum.tile([P, 2, P], F32, tag="wt", bufs=1)
-                for u in range(2):
-                    s = 2 * g + u
-                    nc.tensor.transpose(
-                        w_ps[:, u, :],
-                        uis[:, jb, :].bitcast(F32)[:, s * P : (s + 1) * P],
-                        ident_f[:],
-                    )
-                nc.vector.tensor_copy(
-                    out=wg[:, g, jb * P : (jb + 1) * P, :],
-                    in_=w_ps[:].rearrange("p u j -> p j u"),
-                )
+        ufT = const.tile([P, D, H], BF16)
+        wg = const.tile([P, 6, P, 2], F32, align_bytes=64)
         wcodes = const.tile([P, 2, 3 * H], U32, align_bytes=64)
         wscales = const.tile([P, 2, 3 * H], U8, align_bytes=64)
-        COLS = ((0, 256), (256, 384))
-        for g in range(2):
-            for j0, j1 in COLS:
-                nc.vector.quantize_mx(
-                    out=wcodes[:, g, j0:j1].bitcast(FP8X4),
-                    scales=wscales[:, g, j0:j1],
-                    in_=wg[:, g, j0:j1, :].rearrange("p j u -> p (j u)").bitcast(BF16),
-                )
 
-        xT_tiles = {}
-        gq_tiles = {}
-        code_tiles = {}
-        ca_tiles = {}
-        iou_tiles = {}
+        def ok(t):
+            return 0 <= t < NT
 
-        def transposes_bf16(t):
+        def tb(t):
             c, tt = divmod(t, CH)
-            xt = psum.tile([P, D, P], BF16, tag="xt", bufs=2)
+            xt = psum.tile([P, D, P], BF16, tag="xt", bufs=2, name="xt")
             for d in range(D):
                 nc.tensor.transpose(
                     xt[:, d, :], nh_tiles[c][:, tt, d * H : (d + 1) * H], ident_b[:]
                 )
-            xT = xt_pool.tile([P, D, P], BF16, name="xT")
-            nc.scalar.copy(out=xT[:], in_=xt[:])
-            xT_tiles[t] = xT
+            xt_ps[t] = xt
 
-        def transposes_words(t):
+        def ex(t):
+            xT = xt_pool.tile([P, D, P], BF16, name="xT")
+            nc.scalar.copy(out=xT[:], in_=xt_ps[t][:])
+            xT_sb[t] = xT
+
+        def tw(t):
             c, tt = divmod(t, CH)
-            if tt == 0:
-                gq_tiles[c] = q_pool.tile([P, CH * 512], F32, name="gq", align_bytes=64)
-            wt = psum.tile([P, 4, P], F32, tag="wt", bufs=1)
+            wt = psum.tile([P, 4, P], F32, tag="wt", bufs=1, name="wt")
             words = nh_tiles[c][:, tt, :].bitcast(F32)
             for s in range(4):
                 nc.tensor.transpose(wt[:, s, :], words[:, s * P : (s + 1) * P], ident_f[:])
+            wt_ps[t] = wt
+
+        def ew(t):
+            gq = g_pool.tile([P, 512], F32, name="gq", align_bytes=64)
             nc.scalar.copy(
-                out=gq_tiles[c][:, tt * 512 : (tt + 1) * 512].rearrange(
-                    "p (g n u) -> p g n u", g=2, u=2
-                ),
-                in_=wt[:].rearrange("p (g u) n -> p g n u", u=2),
+                out=gq[:].rearrange("p (g n u) -> p g n u", g=2, u=2),
+                in_=wt_ps[t][:].rearrange("p (g u) n -> p g n u", u=2),
             )
+            gq_sb[t] = gq
 
-        def quantise(c):
-            codes = q_pool.tile([P, CH * 256], U32, name="codes", align_bytes=64)
-            scales = q_pool.tile([P, CH * 256], U8, name="scales", align_bytes=64)
+        def qx(t):
+            codes = q_pool.tile([P, 256], U32, name="codes", align_bytes=64)
+            scales = q_pool.tile([P, 256], U8, name="scales", align_bytes=64)
             nc.vector.quantize_mx(
-                out=codes[:].bitcast(FP8X4), scales=scales[:], in_=gq_tiles[c][:].bitcast(BF16)
+                out=codes[:].bitcast(FP8X4), scales=scales[:], in_=gq_sb[t][:].bitcast(BF16)
             )
-            code_tiles[c] = (codes, scales)
+            code_sb[t] = (codes, scales)
 
-        def forget(t):
-            c, tt = divmod(t, CH)
-            if tt == 0:
-                ca_tiles[c] = fin.tile([P, CH, H], F32, name="ca")
-            xT = xT_tiles[t]
-            zb = z_pool.tile([P, 2, H, 4], F32, name="zb")
+        def fm(t):
+            xT = xT_sb[t]
+            banks = []
             for k in range(2):
-                z = psum.tile([P, 4, H], F32, tag="z", bufs=4)
+                z = psum.tile([P, 4, H], F32, tag="z", bufs=4, name="z")
                 for j in range(4):
                     d = 4 * k + j
                     nc.tensor.matmul(
                         z[:, j, :], lhsT=xT[:, d, :], rhs=ufT[:, d, :], start=True, stop=True
                     )
+                banks.append(z)
+            z_ps[t] = banks
+
+        def ad(t):
+            zb = z_pool.tile([P, 3, H, 4], F32, name="zb")
+            for k in range(2):
                 nc.vector.tensor_tensor(
                     out=zb[:, k, :, :],
-                    in0=z[:].rearrange("p j o -> p o j"),
+                    in0=z_ps[t][k][:].rearrange("p j o -> p o j"),
                     in1=b_all[:, t, :].unsqueeze(2).to_broadcast([P, H, 4]),
                     op=ALU.add,
                 )
-            nc.scalar.activation(out=zb[:], in_=zb[:], func=ACT.Sigmoid)
-            for k in range(2):
-                nc.gpsimd.tensor_tensor(
-                    out=zb[:, k, :, :],
-                    in0=zb[:, k, :, :],
-                    in1=c_tiles[c][:, tt, k * 512 : (k + 1) * 512].rearrange(
-                        "p (j o) -> p o j", j=4
-                    ),
-                    op=ALU.mult,
-                )
+            zb_sb[t] = zb
+
+        def sg(t):
+            zb = zb_sb[t]
+            nc.scalar.activation(out=zb[:, 0:2, :, :], in_=zb[:, 0:2, :, :], func=ACT.Sigmoid)
+
+        def c_view(t, k):
+            c, tt = divmod(t, CH)
+            return c_tiles[c][:, tt, k * 512 : (k + 1) * 512].rearrange("p (j o) -> p o j", j=4)
+
+        def mu1(t):
+            zb = zb_sb[t]
+            nc.vector.tensor_tensor(
+                out=zb[:, 2, :, :], in0=zb[:, 1, :, :], in1=c_view(t, 1), op=ALU.mult
+            )
+
+        def mu0(t):
+            zb = zb_sb[t]
+            nc.gpsimd.tensor_tensor(
+                out=zb[:, 1, :, :], in0=zb[:, 0, :, :], in1=c_view(t, 0), op=ALU.mult
+            )
+
+        def rd(t):
+            c, tt = divmod(t, CH)
+            if tt == 0:
+                ca_sb[c] = fin3.tile([P, CH, H], F32, name="ca")
             nc.vector.tensor_reduce(
-                out=ca_tiles[c][:, tt, :],
-                in_=zb[:].rearrange("p k o j -> p o k j"),
+                out=ca_sb[c][:, tt, :],
+                in_=zb_sb[t][:, 1:3, :, :].rearrange("p k o j -> p o k j"),
                 axis=AX.XY,
                 op=ALU.add,
             )
 
-        def iou_gate(t):
-            c, tt = divmod(t, CH)
-            if tt == 0:
-                iou_tiles[c] = fin.tile([P, CH, 3 * H], F32, name="iou_sb")
-            codes, scales = code_tiles[c]
-            acc = psum.tile([P, 3 * H], F32, tag="iou", bufs=1)
+        def mx(t):
+            codes, scales = code_sb[t]
+            acc = psum.tile([P, 3 * H], F32, tag="iou", bufs=1, name="acc")
             for j0, j1 in COLS:
                 for g in range(2):
-                    n0 = tt * 256 + g * P
                     nc.tensor.matmul_mx(
                         out=acc[:, j0:j1],
-                        lhsT=codes[:, n0 : n0 + P].bitcast(FP8X4),
-                        lhsT_scale=scales[:, n0 : n0 + P],
+                        lhsT=codes[:, g * P : (g + 1) * P].bitcast(FP8X4),
+                        lhsT_scale=scales[:, g * P : (g + 1) * P],
                         rhs=wcodes[:, g, j0:j1].bitcast(FP8X4),
                         rhs_scale=wscales[:, g, j0:j1],
                         start=(g == 0),
                         stop=(g == 1),
                     )
+            acc_ps[t] = acc
+
+        def st(t):
+            c, tt = divmod(t, CH)
+            if tt == 0:
+                iou_sb[c] = fin3.tile([P, CH, 3 * H], F32, name="iou_s")
             nc.vector.scalar_tensor_tensor(
-                out=iou_tiles[c][:, tt, :],
+                out=iou_sb[c][:, tt, :],
                 in0=iou_all[:, t, :],
                 scalar=2.0,
-                in1=acc[:],
+                in1=acc_ps[t][:],
                 op0=ALU.mult,
                 op1=ALU.add,
             )
 
-        def final(c):
-            iou_sb = iou_tiles[c]
-            ts = slice(c * CH, (c + 1) * CH)
-            nc.scalar.activation(
-                out=iou_sb[:, :, 0 : 2 * H], in_=iou_sb[:, :, 0 : 2 * H], func=ACT.Sigmoid
-            )
-            nc.scalar.activation(
-                out=iou_sb[:, :, 2 * H : 3 * H], in_=iou_sb[:, :, 2 * H : 3 * H], func=ACT.Tanh
-            )
-            iu = fin.tile([P, CH, H], F32, name="iu")
-            nc.gpsimd.tensor_tensor(
-                out=iu[:], in0=iou_sb[:, :, 0:H], in1=iou_sb[:, :, 2 * H : 3 * H], op=ALU.mult
-            )
-            c_sb = fin.tile([P, CH, H], F32, name="c_sb")
-            nc.gpsimd.tensor_tensor(out=c_sb[:], in0=iu[:], in1=ca_tiles[c][:], op=ALU.add)
-            nc.sync.dma_start(out=c_out_v[:, ts, :], in_=c_sb[:])
-            tch = fin.tile([P, CH, H], F32, name="tch")
-            nc.scalar.activation(out=tch[:], in_=c_sb[:], func=ACT.Tanh)
-            h_sb = fin.tile([P, CH, H], F32, name="h_sb")
-            nc.gpsimd.tensor_tensor(
-                out=h_sb[:], in0=iou_sb[:, :, H : 2 * H], in1=tch[:], op=ALU.mult
-            )
-            nc.sync.dma_start(out=h_out_v[:, ts, :], in_=h_sb[:])
+        def w_fill(i):
+            wf = psum.tile([P, 2, 2, P], F32, tag="iou", bufs=1, name="wf")
+            for cb in range(2):
+                g, jb = divmod(2 * i + cb, 3)
+                for u in range(2):
+                    s = 2 * g + u
+                    nc.tensor.transpose(
+                        wf[:, cb, u, :],
+                        uis[:, jb, :].bitcast(F32)[:, s * P : (s + 1) * P],
+                        ident_f[:],
+                    )
+            wf_ps[i] = wf
 
-        transposes_bf16(0)
-        for t in range(CH):
-            transposes_words(t)
-        quantise(0)
-        for t in range(NT):
-            c, tt = divmod(t, CH)
-            if tt == 0:
-                if c + 2 < NCH:
-                    load_nh(c + 2)
-                if c + 1 < NCH:
-                    load_c(c + 1)
-            if t + 1 < NT:
-                transposes_bf16(t + 1)
-            if t + CH < NT:
-                transposes_words(t + CH)
-            forget(t)
-            iou_gate(t)
-            if tt == CH - 1:
-                if c + 1 < NCH:
-                    quantise(c + 1)
-                final(c)
+        def w_evac(i):
+            nc.scalar.copy(
+                out=wg[:, 2 * i : 2 * i + 2, :, :],
+                in_=wf_ps[i][:].rearrange("p c u j -> p c j u"),
+            )
+
+        def w_quant():
+            wflat = wg[:].rearrange("p (g b) j u -> p g (b j u)", g=2)
+            for g in range(2):
+                for j0, j1 in COLS:
+                    nc.vector.quantize_mx(
+                        out=wcodes[:, g, j0:j1].bitcast(FP8X4),
+                        scales=wscales[:, g, j0:j1],
+                        in_=wflat[:, g, 2 * j0 : 2 * j1].bitcast(BF16),
+                    )
+
+        def tail_engine(c):
+            return nc.vector if c == NCH - 1 else nc.gpsimd
+
+        def fin_st(c):
+            s = iou_sb[c]
+            nc.scalar.activation(out=s[:, :, 0 : 2 * H], in_=s[:, :, 0 : 2 * H], func=ACT.Sigmoid)
+            nc.scalar.activation(
+                out=s[:, :, 2 * H : 3 * H], in_=s[:, :, 2 * H : 3 * H], func=ACT.Tanh
+            )
+
+        def f1(c):
+            s = iou_sb[c]
+            iu_sb[c] = fin.tile([P, CH, H], F32, name="iu")
+            tail_engine(c).tensor_tensor(
+                out=iu_sb[c][:], in0=s[:, :, 0:H], in1=s[:, :, 2 * H : 3 * H], op=ALU.mult
+            )
+
+        def f2(c):
+            c_sb[c] = fin.tile([P, CH, H], F32, name="c_o")
+            tail_engine(c).tensor_tensor(
+                out=c_sb[c][:], in0=iu_sb[c][:], in1=ca_sb[c][:], op=ALU.add
+            )
+            nc.sync.dma_start(out=c_out_v[:, c * CH : (c + 1) * CH, :], in_=c_sb[c][:])
+
+        def fin2(c):
+            tch_sb[c] = fin.tile([P, CH, H], F32, name="tch")
+            nc.scalar.activation(out=tch_sb[c][:], in_=c_sb[c][:], func=ACT.Tanh)
+
+        def f3(c):
+            h_sb[c] = fin.tile([P, CH, H], F32, name="h_o")
+            tail_engine(c).tensor_tensor(
+                out=h_sb[c][:], in0=iou_sb[c][:, :, H : 2 * H], in1=tch_sb[c][:], op=ALU.mult
+            )
+            nc.sync.dma_start(out=h_out_v[:, c * CH : (c + 1) * CH, :], in_=h_sb[c][:])
+
+        for r in range(-5, fin_base(NCH - 1) + 3):
+            if r >= 0 and r % CH == 0:
+                m = r // CH
+                if m + 3 < NCH:
+                    alloc_nh(m + 3)
+                    load_nh(m + 3, 0, CH)
+                if m + 2 < NCH:
+                    alloc_c(m + 2)
+                    load_c(m + 2, 0, CH)
+            sts = st_rounds.get(r, [])
+            nxt = st_rounds.get(r + 1, [])
+            if ok(r + 2):
+                qx(r + 2)
+            if r == RHO0 - 1:
+                w_quant()
+            if ok(r):
+                mu1(r)
+            if sts:
+                st(sts[0])
+            if ok(r):
+                mu0(r)
+            if ok(r + 3):
+                ew(r + 3)
+            if ok(r + 4):
+                ex(r + 4)
+            if ok(r + 1):
+                sg(r + 1)
+            if RHO0 - 4 <= r < RHO0 - 1:
+                w_evac(r - (RHO0 - 4))
+            for c in range(NCH):
+                if fin_base(c) == r:
+                    fin_st(c)
+                if fin_base(c) + 2 == r:
+                    fin2(c)
+            if len(sts) > 1:
+                mx(sts[1])
+            if ok(r + 3):
+                fm(r + 3)
+            if ok(r + 5):
+                tb(r + 5)
+            if r == -5:
+                uf_ps = psum.tile([P, D, H], BF16, tag="xt", bufs=2, name="uf_ps")
+                for d in range(D):
+                    nc.tensor.transpose(uf_ps[:, d, :], ufs[:, d, :], ident_b[:])
+                nc.vector.tensor_copy(out=ufT[:], in_=uf_ps[:])
+            if ok(r + 4):
+                tw(r + 4)
+            if RHO0 - 5 <= r < RHO0 - 2:
+                w_fill(r - (RHO0 - 5))
+            if ok(r + 2):
+                ad(r + 2)
+            if ok(r - 1):
+                rd(r - 1)
+            if len(sts) > 1:
+                st(sts[1])
+            if nxt:
+                mx(nxt[0])
+            for c in range(NCH):
+                if fin_base(c) == r:
+                    f1(c)
+                if fin_base(c) + 1 == r:
+                    f2(c)
+                if fin_base(c) + 2 == r:
+                    f3(c)

@@ -21,6 +21,7 @@ CH = 4
 NCH = NT // CH
 RHO0 = 6
 COLS = ((0, 256), (256, 384))
+PE_ADD = (1, 4, 6)
 
 FLOPS = 2 * N_NODES * D * H * 3 * H + 2 * N_NODES * D * H * H
 
@@ -138,6 +139,9 @@ def tile_generictreelstmcell_t_kernel(
         def ok(t):
             return 0 <= t < NT
 
+        def pe_adds(t):
+            return t % 8 in PE_ADD
+
         def tb(t):
             c, tt = divmod(t, CH)
             xt = psum.tile([P, D, P], BF16, tag="xt", bufs=2, name="xt")
@@ -181,43 +185,73 @@ def tile_generictreelstmcell_t_kernel(
             banks = []
             for k in range(2):
                 z = psum.tile([P, 4, H], F32, tag="z", bufs=4, name="z")
+                by_pe = pe_adds(t) and k == 0
+                if by_pe:
+                    nc.tensor.matmul(
+                        z[:],
+                        lhsT=ident_b[:],
+                        rhs=b_all[:, t, :].unsqueeze(1).to_broadcast([P, 4, H]),
+                        start=True,
+                        stop=False,
+                    )
                 for j in range(4):
                     d = 4 * k + j
                     nc.tensor.matmul(
-                        z[:, j, :], lhsT=xT[:, d, :], rhs=ufT[:, d, :], start=True, stop=True
+                        z[:, j, :],
+                        lhsT=xT[:, d, :],
+                        rhs=ufT[:, d, :],
+                        start=not by_pe,
+                        stop=(not by_pe) or j == 3,
                     )
                 banks.append(z)
             z_ps[t] = banks
 
         def ad(t):
-            zb = z_pool.tile([P, 3, H, 4], F32, name="zb")
-            for k in range(2):
+            zb = z_pool.tile([P, 5, H, 2], F32, name="zb")
+            for k in range(1 if pe_adds(t) else 0, 2):
                 nc.vector.tensor_tensor(
-                    out=zb[:, k, :, :],
-                    in0=z_ps[t][k][:].rearrange("p j o -> p o j"),
-                    in1=b_all[:, t, :].unsqueeze(2).to_broadcast([P, H, 4]),
+                    out=zb[:, 2 * k : 2 * k + 2, :, :],
+                    in0=z_ps[t][k][:].rearrange("p (q e) o -> p q o e", e=2),
+                    in1=b_all[:, t, :].unsqueeze(1).unsqueeze(3).to_broadcast([P, 2, H, 2]),
                     op=ALU.add,
                 )
             zb_sb[t] = zb
 
         def sg(t):
             zb = zb_sb[t]
-            nc.scalar.activation(out=zb[:, 0:2, :, :], in_=zb[:, 0:2, :, :], func=ACT.Sigmoid)
+            if pe_adds(t):
+                nc.scalar.activation(
+                    out=zb[:, 0:2, :, :],
+                    in_=z_ps[t][0][:].rearrange("p (q e) o -> p q o e", e=2),
+                    func=ACT.Sigmoid,
+                )
+                nc.scalar.activation(
+                    out=zb[:, 2:4, :, :], in_=zb[:, 2:4, :, :], func=ACT.Sigmoid
+                )
+            else:
+                nc.scalar.activation(
+                    out=zb[:, 0:4, :, :], in_=zb[:, 0:4, :, :], func=ACT.Sigmoid
+                )
 
-        def c_view(t, k):
+        def c_view(t, q0, q1):
             c, tt = divmod(t, CH)
-            return c_tiles[c][:, tt, k * 512 : (k + 1) * 512].rearrange("p (j o) -> p o j", j=4)
+            return c_tiles[c][:, tt, q0 * 256 : q1 * 256].rearrange(
+                "p (q e o) -> p q o e", e=2, o=H
+            )
 
         def mu1(t):
             zb = zb_sb[t]
             nc.vector.tensor_tensor(
-                out=zb[:, 2, :, :], in0=zb[:, 1, :, :], in1=c_view(t, 1), op=ALU.mult
+                out=zb[:, 4:5, :, :], in0=zb[:, 3:4, :, :], in1=c_view(t, 3, 4), op=ALU.mult
             )
 
         def mu0(t):
             zb = zb_sb[t]
             nc.gpsimd.tensor_tensor(
-                out=zb[:, 1, :, :], in0=zb[:, 0, :, :], in1=c_view(t, 0), op=ALU.mult
+                out=zb[:, 3:4, :, :], in0=zb[:, 0:1, :, :], in1=c_view(t, 0, 1), op=ALU.mult
+            )
+            nc.gpsimd.tensor_tensor(
+                out=zb[:, 1:3, :, :], in0=zb[:, 1:3, :, :], in1=c_view(t, 1, 3), op=ALU.mult
             )
 
         def rd(t):
@@ -226,7 +260,7 @@ def tile_generictreelstmcell_t_kernel(
                 ca_sb[c] = fin3.tile([P, CH, H], F32, name="ca")
             nc.vector.tensor_reduce(
                 out=ca_sb[c][:, tt, :],
-                in_=zb_sb[t][:, 1:3, :, :].rearrange("p k o j -> p o k j"),
+                in_=zb_sb[t][:, 1:5, :, :].rearrange("p q o e -> p o q e"),
                 axis=AX.XY,
                 op=ALU.add,
             )

@@ -207,7 +207,7 @@ def tile_generictreelstmcell_t_kernel(
             z_ps[t] = banks
 
         def ad(t):
-            zb = z_pool.tile([P, 5, H, 2], F32, name="zb")
+            zb = z_pool.tile([P, 6, H, 2], F32, name="zb")
             for k in range(1 if pe_adds(t) else 0, 2):
                 nc.vector.tensor_tensor(
                     out=zb[:, 2 * k : 2 * k + 2, :, :],
@@ -242,16 +242,14 @@ def tile_generictreelstmcell_t_kernel(
         def mu1(t):
             zb = zb_sb[t]
             nc.vector.tensor_tensor(
-                out=zb[:, 4:5, :, :], in0=zb[:, 3:4, :, :], in1=c_view(t, 3, 4), op=ALU.mult
+                out=zb[:, 4:6, :, :], in0=zb[:, 2:4, :, :], in1=c_view(t, 2, 4), op=ALU.mult
             )
 
         def mu0(t):
             zb = zb_sb[t]
-            nc.gpsimd.tensor_tensor(
-                out=zb[:, 3:4, :, :], in0=zb[:, 0:1, :, :], in1=c_view(t, 0, 1), op=ALU.mult
-            )
-            nc.gpsimd.tensor_tensor(
-                out=zb[:, 1:3, :, :], in0=zb[:, 1:3, :, :], in1=c_view(t, 1, 3), op=ALU.mult
+            eng = nc.vector if t >= NT - 2 else nc.gpsimd
+            eng.tensor_tensor(
+                out=zb[:, 2:4, :, :], in0=zb[:, 0:2, :, :], in1=c_view(t, 0, 2), op=ALU.mult
             )
 
         def rd(t):
@@ -260,7 +258,7 @@ def tile_generictreelstmcell_t_kernel(
                 ca_sb[c] = fin3.tile([P, CH, H], F32, name="ca")
             nc.vector.tensor_reduce(
                 out=ca_sb[c][:, tt, :],
-                in_=zb_sb[t][:, 1:5, :, :].rearrange("p q o e -> p o q e"),
+                in_=zb_sb[t][:, 2:6, :, :].rearrange("p q o e -> p o q e"),
                 axis=AX.XY,
                 op=ALU.add,
             )

@@ -21,7 +21,7 @@ CH = 4
 NCH = NT // CH
 RHO0 = 6
 COLS = ((0, 256), (256, 384))
-PE_ADD = (1, 4, 6)
+B_GROUPS = ((0, 4), (4, 12), (12, 20), (20, 28), (28, 32))
 
 FLOPS = 2 * N_NODES * D * H * 3 * H + 2 * N_NODES * D * H * H
 
@@ -79,6 +79,7 @@ def tile_generictreelstmcell_t_kernel(
         tch_sb = {}
         h_sb = {}
         wf_ps = {}
+        bt_ps = {}
 
         def alloc_nh(c):
             nh_tiles[c] = nh_pool.tile([P, CH, D * H], BF16, name="nh_sb")
@@ -115,6 +116,7 @@ def tile_generictreelstmcell_t_kernel(
         load_nh(0, 1, CH)
         alloc_c(0)
         load_c(0, 0, 1)
+        nc.sync.dma_start(out=b_all[:, 4:12, :], in_=b_v[:, 4:12, :])
         alloc_nh(1)
         load_nh(1, 0, CH)
         load_c(0, 1, CH)
@@ -124,7 +126,7 @@ def tile_generictreelstmcell_t_kernel(
                 in_=U_iou[:, jb * P : (jb + 1) * P, :].rearrange("d j h -> j d h"),
             )
         nc.sync.dma_start(out=iou_all[:, 0:8, :], in_=iou_v[:, 0:8, :])
-        nc.sync.dma_start(out=b_all[:, CH:NT, :], in_=b_v[:, CH:NT, :])
+        nc.sync.dma_start(out=b_all[:, 12:NT, :], in_=b_v[:, 12:NT, :])
         alloc_c(1)
         load_c(1, 0, CH)
         alloc_nh(2)
@@ -132,6 +134,7 @@ def tile_generictreelstmcell_t_kernel(
         nc.sync.dma_start(out=iou_all[:, 8:NT, :], in_=iou_v[:, 8:NT, :])
 
         ufT = const.tile([P, D, H], BF16)
+        bT = const.tile([P, NT, P], F32)
         wg = const.tile([P, 6, P, 2], F32, align_bytes=64)
         wcodes = const.tile([P, 2, 3 * H], U32, align_bytes=64)
         wscales = const.tile([P, 2, 3 * H], U8, align_bytes=64)
@@ -139,8 +142,16 @@ def tile_generictreelstmcell_t_kernel(
         def ok(t):
             return 0 <= t < NT
 
-        def pe_adds(t):
-            return t % 8 in PE_ADD
+        def bt_fill(g):
+            t0, t1 = B_GROUPS[g]
+            ps = psum.tile([P, D, P], BF16, tag="xt", bufs=2, name="bt")
+            for i in range(t1 - t0):
+                nc.tensor.transpose(ps[:, i, :], b_all[:, t0 + i, :], ident_b[:])
+            bt_ps[g] = ps
+
+        def bt_evac(g):
+            t0, t1 = B_GROUPS[g]
+            nc.vector.tensor_copy(out=bT[:, t0:t1, :], in_=bt_ps[g][:, 0 : t1 - t0, :])
 
         def tb(t):
             c, tt = divmod(t, CH)
@@ -185,53 +196,37 @@ def tile_generictreelstmcell_t_kernel(
             banks = []
             for k in range(2):
                 z = psum.tile([P, 4, H], F32, tag="z", bufs=4, name="z")
-                by_pe = pe_adds(t) and k == 0
-                if by_pe:
+                for j in range(4):
                     nc.tensor.matmul(
-                        z[:],
-                        lhsT=ident_b[:],
-                        rhs=b_all[:, t, :].unsqueeze(1).to_broadcast([P, 4, H]),
-                        start=True,
+                        z[:, j, :],
+                        lhsT=bT[:, t, :],
+                        rhs=ident_f[:],
+                        start=(j == 0),
                         stop=False,
+                        is_transpose=True,
                     )
+                banks.append(z)
+            for k in range(2):
                 for j in range(4):
                     d = 4 * k + j
                     nc.tensor.matmul(
-                        z[:, j, :],
+                        banks[k][:, j, :],
                         lhsT=xT[:, d, :],
                         rhs=ufT[:, d, :],
-                        start=not by_pe,
-                        stop=(not by_pe) or j == 3,
+                        start=False,
+                        stop=(j == 3),
                     )
-                banks.append(z)
             z_ps[t] = banks
 
-        def ad(t):
-            zb = z_pool.tile([P, 6, H, 2], F32, name="zb")
-            for k in range(1 if pe_adds(t) else 0, 2):
-                nc.vector.tensor_tensor(
-                    out=zb[:, 2 * k : 2 * k + 2, :, :],
-                    in0=z_ps[t][k][:].rearrange("p (q e) o -> p q o e", e=2),
-                    in1=b_all[:, t, :].unsqueeze(1).unsqueeze(3).to_broadcast([P, 2, H, 2]),
-                    op=ALU.add,
-                )
-            zb_sb[t] = zb
-
         def sg(t):
-            zb = zb_sb[t]
-            if pe_adds(t):
+            zb = z_pool.tile([P, 4, H, 2], F32, name="zb")
+            for k in range(2):
                 nc.scalar.activation(
-                    out=zb[:, 0:2, :, :],
-                    in_=z_ps[t][0][:].rearrange("p (q e) o -> p q o e", e=2),
+                    out=zb[:, 2 * k : 2 * k + 2, :, :],
+                    in_=z_ps[t][k][:].rearrange("p (q e) o -> p q o e", e=2),
                     func=ACT.Sigmoid,
                 )
-                nc.scalar.activation(
-                    out=zb[:, 2:4, :, :], in_=zb[:, 2:4, :, :], func=ACT.Sigmoid
-                )
-            else:
-                nc.scalar.activation(
-                    out=zb[:, 0:4, :, :], in_=zb[:, 0:4, :, :], func=ACT.Sigmoid
-                )
+            zb_sb[t] = zb
 
         def c_view(t, q0, q1):
             c, tt = divmod(t, CH)
@@ -239,18 +234,9 @@ def tile_generictreelstmcell_t_kernel(
                 "p (q e o) -> p q o e", e=2, o=H
             )
 
-        def mu1(t):
+        def mu(t):
             zb = zb_sb[t]
-            nc.vector.tensor_tensor(
-                out=zb[:, 4:6, :, :], in0=zb[:, 2:4, :, :], in1=c_view(t, 2, 4), op=ALU.mult
-            )
-
-        def mu0(t):
-            zb = zb_sb[t]
-            eng = nc.vector if t >= NT - 2 else nc.gpsimd
-            eng.tensor_tensor(
-                out=zb[:, 2:4, :, :], in0=zb[:, 0:2, :, :], in1=c_view(t, 0, 2), op=ALU.mult
-            )
+            nc.vector.tensor_tensor(out=zb[:], in0=zb[:], in1=c_view(t, 0, 4), op=ALU.mult)
 
         def rd(t):
             c, tt = divmod(t, CH)
@@ -258,7 +244,7 @@ def tile_generictreelstmcell_t_kernel(
                 ca_sb[c] = fin3.tile([P, CH, H], F32, name="ca")
             nc.vector.tensor_reduce(
                 out=ca_sb[c][:, tt, :],
-                in_=zb_sb[t][:, 2:6, :, :].rearrange("p q o e -> p o q e"),
+                in_=zb_sb[t][:].rearrange("p q o e -> p o q e"),
                 axis=AX.XY,
                 op=ALU.add,
             )
@@ -371,18 +357,16 @@ def tile_generictreelstmcell_t_kernel(
                 qx(r + 2)
             if r == RHO0 - 1:
                 w_quant()
-            if ok(r):
-                mu1(r)
+            if ok(r + 1):
+                mu(r + 1)
             if sts:
                 st(sts[0])
-            if ok(r):
-                mu0(r)
             if ok(r + 3):
                 ew(r + 3)
             if ok(r + 4):
                 ex(r + 4)
-            if ok(r + 1):
-                sg(r + 1)
+            if ok(r + 2):
+                sg(r + 2)
             if RHO0 - 4 <= r < RHO0 - 1:
                 w_evac(r - (RHO0 - 4))
             for c in range(NCH):
@@ -401,14 +385,16 @@ def tile_generictreelstmcell_t_kernel(
                 for d in range(D):
                     nc.tensor.transpose(uf_ps[:, d, :], ufs[:, d, :], ident_b[:])
                 nc.vector.tensor_copy(out=ufT[:], in_=uf_ps[:])
+            for g in range(len(B_GROUPS)):
+                if max(B_GROUPS[g][0] - 5, -4) == r:
+                    bt_fill(g)
+                    bt_evac(g)
             if ok(r + 4):
                 tw(r + 4)
             if RHO0 - 5 <= r < RHO0 - 2:
                 w_fill(r - (RHO0 - 5))
-            if ok(r + 2):
-                ad(r + 2)
-            if ok(r - 1):
-                rd(r - 1)
+            if ok(r):
+                rd(r)
             if len(sts) > 1:
                 st(sts[1])
             if nxt:

@@ -19,19 +19,11 @@ H = 128
 NT = N_NODES // P
 CH = 4
 NCH = NT // CH
-RHO0 = 6
 COLS = ((0, 256), (256, 384))
-B_GROUPS = ((0, 4), (4, 12), (12, 20), (20, 28), (28, 32))
+BG = 4
+W_READY = 4
 
 FLOPS = 2 * N_NODES * D * H * 3 * H + 2 * N_NODES * D * H * H
-
-
-def rho(t):
-    return max(t, RHO0 + t // 2)
-
-
-def fin_base(c):
-    return max(CH * c + CH, rho(CH * c + CH - 1) + 1)
 
 
 def tile_generictreelstmcell_t_kernel(
@@ -45,10 +37,6 @@ def tile_generictreelstmcell_t_kernel(
     h_out_v = out_0.rearrange("(p t) o -> p t o", t=NT)
     c_out_v = out_1.rearrange("(p t) o -> p t o", t=NT)
 
-    st_rounds = {}
-    for t in range(NT):
-        st_rounds[rho(t)] = st_rounds.get(rho(t), []) + [t]
-
     with ExitStack() as ctx:
         const = ctx.enter_context(tc.tile_pool(name="const", bufs=1))
         nh_pool = ctx.enter_context(tc.tile_pool(name="nh", bufs=3))
@@ -57,10 +45,12 @@ def tile_generictreelstmcell_t_kernel(
         g_pool = ctx.enter_context(tc.tile_pool(name="grp", bufs=3))
         q_pool = ctx.enter_context(tc.tile_pool(name="quant", bufs=10))
         z_pool = ctx.enter_context(tc.tile_pool(name="zb", bufs=4))
-        fin3 = ctx.enter_context(tc.tile_pool(name="fin3", bufs=3))
-        fin = ctx.enter_context(tc.tile_pool(name="fin", bufs=2))
-        psum = ctx.enter_context(tc.psum_pool(name="psum", bufs=1))
+        fin = ctx.enter_context(tc.tile_pool(name="fin", bufs=4))
+        psum = ctx.enter_context(tc.psum_pool(name="psum", bufs=8))
         ctx.enter_context(tc.manual_schedule())
+
+        def bank(shape, dtype):
+            return psum.tile(shape, dtype, tag="ring", bufs=8, name="ring")
 
         nh_tiles = {}
         c_tiles = {}
@@ -113,24 +103,25 @@ def tile_generictreelstmcell_t_kernel(
         load_nh(0, 0, 1)
         nc.sync.dma_start(out=ufs[:], in_=U_f.rearrange("d o h -> o d h"))
         nc.sync.dma_start(out=b_all[:, 0:CH, :], in_=b_v[:, 0:CH, :])
-        load_nh(0, 1, CH)
+        load_nh(0, 1, 2)
         alloc_c(0)
         load_c(0, 0, 1)
-        nc.sync.dma_start(out=b_all[:, 4:12, :], in_=b_v[:, 4:12, :])
-        alloc_nh(1)
-        load_nh(1, 0, CH)
-        load_c(0, 1, CH)
         for jb in range(3):
             nc.sync.dma_start(
                 out=uis[:, jb, :].rearrange("p (d h) -> p d h", d=D),
                 in_=U_iou[:, jb * P : (jb + 1) * P, :].rearrange("d j h -> j d h"),
             )
+        load_nh(0, 2, CH)
+        load_c(0, 1, CH)
         nc.sync.dma_start(out=iou_all[:, 0:8, :], in_=iou_v[:, 0:8, :])
-        nc.sync.dma_start(out=b_all[:, 12:NT, :], in_=b_v[:, 12:NT, :])
+        alloc_nh(1)
+        load_nh(1, 0, CH)
+        nc.sync.dma_start(out=b_all[:, 4:12, :], in_=b_v[:, 4:12, :])
         alloc_c(1)
         load_c(1, 0, CH)
         alloc_nh(2)
         load_nh(2, 0, CH)
+        nc.sync.dma_start(out=b_all[:, 12:NT, :], in_=b_v[:, 12:NT, :])
         nc.sync.dma_start(out=iou_all[:, 8:NT, :], in_=iou_v[:, 8:NT, :])
 
         ufT = const.tile([P, D, H], BF16)
@@ -142,20 +133,24 @@ def tile_generictreelstmcell_t_kernel(
         def ok(t):
             return 0 <= t < NT
 
+        def uf_fill():
+            uf_ps = bank([P, D, H], BF16)
+            for d in range(D):
+                nc.tensor.transpose(uf_ps[:, d, :], ufs[:, d, :], ident_b[:])
+            nc.vector.tensor_copy(out=ufT[:], in_=uf_ps[:])
+
         def bt_fill(g):
-            t0, t1 = B_GROUPS[g]
-            ps = psum.tile([P, D, P], BF16, tag="xt", bufs=2, name="bt")
-            for i in range(t1 - t0):
-                nc.tensor.transpose(ps[:, i, :], b_all[:, t0 + i, :], ident_b[:])
+            ps = bank([P, BG, P], BF16)
+            for i in range(BG):
+                nc.tensor.transpose(ps[:, i, :], b_all[:, BG * g + i, :], ident_b[:])
             bt_ps[g] = ps
 
         def bt_evac(g):
-            t0, t1 = B_GROUPS[g]
-            nc.vector.tensor_copy(out=bT[:, t0:t1, :], in_=bt_ps[g][:, 0 : t1 - t0, :])
+            nc.scalar.copy(out=bT[:, BG * g : BG * (g + 1), :], in_=bt_ps[g][:])
 
         def tb(t):
             c, tt = divmod(t, CH)
-            xt = psum.tile([P, D, P], BF16, tag="xt", bufs=2, name="xt")
+            xt = bank([P, D, P], BF16)
             for d in range(D):
                 nc.tensor.transpose(
                     xt[:, d, :], nh_tiles[c][:, tt, d * H : (d + 1) * H], ident_b[:]
@@ -169,7 +164,7 @@ def tile_generictreelstmcell_t_kernel(
 
         def tw(t):
             c, tt = divmod(t, CH)
-            wt = psum.tile([P, 4, P], F32, tag="wt", bufs=1, name="wt")
+            wt = bank([P, 4, P], F32)
             words = nh_tiles[c][:, tt, :].bitcast(F32)
             for s in range(4):
                 nc.tensor.transpose(wt[:, s, :], words[:, s * P : (s + 1) * P], ident_f[:])
@@ -195,7 +190,7 @@ def tile_generictreelstmcell_t_kernel(
             xT = xT_sb[t]
             banks = []
             for k in range(2):
-                z = psum.tile([P, 4, H], F32, tag="z", bufs=4, name="z")
+                z = bank([P, 4, H], F32)
                 for j in range(4):
                     nc.tensor.matmul(
                         z[:, j, :],
@@ -228,20 +223,20 @@ def tile_generictreelstmcell_t_kernel(
                 )
             zb_sb[t] = zb
 
-        def c_view(t, q0, q1):
-            c, tt = divmod(t, CH)
-            return c_tiles[c][:, tt, q0 * 256 : q1 * 256].rearrange(
-                "p (q e o) -> p q o e", e=2, o=H
-            )
-
         def mu(t):
+            c, tt = divmod(t, CH)
             zb = zb_sb[t]
-            nc.vector.tensor_tensor(out=zb[:], in0=zb[:], in1=c_view(t, 0, 4), op=ALU.mult)
+            nc.vector.tensor_tensor(
+                out=zb[:],
+                in0=zb[:],
+                in1=c_tiles[c][:, tt, :].rearrange("p (q e o) -> p q o e", e=2, o=H),
+                op=ALU.mult,
+            )
 
         def rd(t):
             c, tt = divmod(t, CH)
             if tt == 0:
-                ca_sb[c] = fin3.tile([P, CH, H], F32, name="ca")
+                ca_sb[c] = fin.tile([P, CH, H], F32, name="ca")
             nc.vector.tensor_reduce(
                 out=ca_sb[c][:, tt, :],
                 in_=zb_sb[t][:].rearrange("p q o e -> p o q e"),
@@ -251,7 +246,7 @@ def tile_generictreelstmcell_t_kernel(
 
         def mx(t):
             codes, scales = code_sb[t]
-            acc = psum.tile([P, 3 * H], F32, tag="iou", bufs=1, name="acc")
+            acc = bank([P, 3 * H], F32)
             for j0, j1 in COLS:
                 for g in range(2):
                     nc.tensor.matmul_mx(
@@ -268,7 +263,7 @@ def tile_generictreelstmcell_t_kernel(
         def st(t):
             c, tt = divmod(t, CH)
             if tt == 0:
-                iou_sb[c] = fin3.tile([P, CH, 3 * H], F32, name="iou_s")
+                iou_sb[c] = fin.tile([P, CH, 3 * H], F32, name="iou_s")
             nc.vector.scalar_tensor_tensor(
                 out=iou_sb[c][:, tt, :],
                 in0=iou_all[:, t, :],
@@ -279,7 +274,7 @@ def tile_generictreelstmcell_t_kernel(
             )
 
         def w_fill(i):
-            wf = psum.tile([P, 2, 2, P], F32, tag="iou", bufs=1, name="wf")
+            wf = bank([P, 2, 2, P], F32)
             for cb in range(2):
                 g, jb = divmod(2 * i + cb, 3)
                 for u in range(2):
@@ -307,102 +302,113 @@ def tile_generictreelstmcell_t_kernel(
                         in_=wflat[:, g, 2 * j0 : 2 * j1].bitcast(BF16),
                     )
 
-        def tail_engine(c):
-            return nc.vector if c == NCH - 1 else nc.gpsimd
-
-        def fin_st(c):
+        def fa(t):
+            c, tt = divmod(t, CH)
             s = iou_sb[c]
-            nc.scalar.activation(out=s[:, :, 0 : 2 * H], in_=s[:, :, 0 : 2 * H], func=ACT.Sigmoid)
             nc.scalar.activation(
-                out=s[:, :, 2 * H : 3 * H], in_=s[:, :, 2 * H : 3 * H], func=ACT.Tanh
+                out=s[:, tt, 0 : 2 * H], in_=s[:, tt, 0 : 2 * H], func=ACT.Sigmoid
+            )
+            nc.scalar.activation(
+                out=s[:, tt, 2 * H : 3 * H], in_=s[:, tt, 2 * H : 3 * H], func=ACT.Tanh
             )
 
-        def f1(c):
+        def f1(t):
+            c, tt = divmod(t, CH)
             s = iou_sb[c]
-            iu_sb[c] = fin.tile([P, CH, H], F32, name="iu")
-            tail_engine(c).tensor_tensor(
-                out=iu_sb[c][:], in0=s[:, :, 0:H], in1=s[:, :, 2 * H : 3 * H], op=ALU.mult
+            if tt == 0:
+                iu_sb[c] = fin.tile([P, CH, H], F32, name="iu")
+            nc.vector.tensor_tensor(
+                out=iu_sb[c][:, tt, :], in0=s[:, tt, 0:H], in1=s[:, tt, 2 * H : 3 * H], op=ALU.mult
             )
 
-        def f2(c):
-            c_sb[c] = fin.tile([P, CH, H], F32, name="c_o")
-            tail_engine(c).tensor_tensor(
-                out=c_sb[c][:], in0=iu_sb[c][:], in1=ca_sb[c][:], op=ALU.add
+        def f2(t):
+            c, tt = divmod(t, CH)
+            if tt == 0:
+                c_sb[c] = fin.tile([P, CH, H], F32, name="c_o")
+            nc.vector.tensor_tensor(
+                out=c_sb[c][:, tt, :], in0=iu_sb[c][:, tt, :], in1=ca_sb[c][:, tt, :], op=ALU.add
             )
-            nc.sync.dma_start(out=c_out_v[:, c * CH : (c + 1) * CH, :], in_=c_sb[c][:])
+            if tt == CH - 1:
+                nc.sync.dma_start(out=c_out_v[:, c * CH : (c + 1) * CH, :], in_=c_sb[c][:])
 
-        def fin2(c):
-            tch_sb[c] = fin.tile([P, CH, H], F32, name="tch")
-            nc.scalar.activation(out=tch_sb[c][:], in_=c_sb[c][:], func=ACT.Tanh)
+        def fb(t):
+            c, tt = divmod(t, CH)
+            if tt == 0:
+                tch_sb[c] = fin.tile([P, CH, H], F32, name="tch")
+            nc.scalar.activation(out=tch_sb[c][:, tt, :], in_=c_sb[c][:, tt, :], func=ACT.Tanh)
 
-        def f3(c):
-            h_sb[c] = fin.tile([P, CH, H], F32, name="h_o")
-            tail_engine(c).tensor_tensor(
-                out=h_sb[c][:], in0=iou_sb[c][:, :, H : 2 * H], in1=tch_sb[c][:], op=ALU.mult
+        def f3(t):
+            c, tt = divmod(t, CH)
+            if tt == 0:
+                h_sb[c] = fin.tile([P, CH, H], F32, name="h_o")
+            nc.vector.tensor_tensor(
+                out=h_sb[c][:, tt, :], in0=iou_sb[c][:, tt, H : 2 * H], in1=tch_sb[c][:, tt, :], op=ALU.mult
             )
-            nc.sync.dma_start(out=h_out_v[:, c * CH : (c + 1) * CH, :], in_=h_sb[c][:])
+            if tt == CH - 1:
+                nc.sync.dma_start(out=h_out_v[:, c * CH : (c + 1) * CH, :], in_=h_sb[c][:])
 
-        for r in range(-5, fin_base(NCH - 1) + 3):
-            if r >= 0 and r % CH == 0:
-                m = r // CH
+        def m_round(t):
+            return max(t + 3, W_READY + 1 + t // 2)
+
+        by_round = {}
+        for t in range(NT):
+            by_round.setdefault(m_round(t), []).append(t)
+
+        def late(r, k):
+            return by_round.get(r - k, [])
+
+        for r in range(0, m_round(NT - 1) + 6):
+            if r >= 5 and (r - 5) % CH == 0:
+                m = (r - 5) // CH
                 if m + 3 < NCH:
                     alloc_nh(m + 3)
                     load_nh(m + 3, 0, CH)
                 if m + 2 < NCH:
                     alloc_c(m + 2)
                     load_c(m + 2, 0, CH)
-            sts = st_rounds.get(r, [])
-            nxt = st_rounds.get(r + 1, [])
-            if ok(r + 2):
-                qx(r + 2)
-            if r == RHO0 - 1:
-                w_quant()
-            if ok(r + 1):
-                mu(r + 1)
-            if sts:
-                st(sts[0])
-            if ok(r + 3):
-                ew(r + 3)
-            if ok(r + 4):
-                ex(r + 4)
-            if ok(r + 2):
-                sg(r + 2)
-            if RHO0 - 4 <= r < RHO0 - 1:
-                w_evac(r - (RHO0 - 4))
-            for c in range(NCH):
-                if fin_base(c) == r:
-                    fin_st(c)
-                if fin_base(c) + 2 == r:
-                    fin2(c)
-            if len(sts) > 1:
-                mx(sts[1])
-            if ok(r + 3):
-                fm(r + 3)
-            if ok(r + 5):
-                tb(r + 5)
-            if r == -5:
-                uf_ps = psum.tile([P, D, H], BF16, tag="xt", bufs=2, name="uf_ps")
-                for d in range(D):
-                    nc.tensor.transpose(uf_ps[:, d, :], ufs[:, d, :], ident_b[:])
-                nc.vector.tensor_copy(out=ufT[:], in_=uf_ps[:])
-            for g in range(len(B_GROUPS)):
-                if max(B_GROUPS[g][0] - 5, -4) == r:
-                    bt_fill(g)
+            if ok(r - 3):
+                sg(r - 3)
+            for t in late(r, 2):
+                fa(t)
+            for t in late(r, 4):
+                fb(t)
+            if ok(r - 1):
+                ex(r - 1)
+                ew(r - 1)
+            for g in range(NT // BG):
+                if max(BG * g, 1) == r:
                     bt_evac(g)
-            if ok(r + 4):
-                tw(r + 4)
-            if RHO0 - 5 <= r < RHO0 - 2:
-                w_fill(r - (RHO0 - 5))
+            if r == W_READY - 1:
+                for i in range(3):
+                    w_evac(i)
+            if ok(r - 4):
+                mu(r - 4)
+            for t in late(r, 1):
+                st(t)
+            if ok(r - 2):
+                qx(r - 2)
+            if r == W_READY:
+                w_quant()
+            for t in late(r, 3):
+                f1(t)
+                f2(t)
+            for t in late(r, 5):
+                f3(t)
+            if ok(r - 5):
+                rd(r - 5)
+            if ok(r - 2):
+                fm(r - 2)
+            for t in late(r, 0):
+                mx(t)
+            if r == W_READY - 2:
+                for i in range(3):
+                    w_fill(i)
             if ok(r):
-                rd(r)
-            if len(sts) > 1:
-                st(sts[1])
-            if nxt:
-                mx(nxt[0])
-            for c in range(NCH):
-                if fin_base(c) == r:
-                    f1(c)
-                if fin_base(c) + 1 == r:
-                    f2(c)
-                if fin_base(c) + 2 == r:
-                    f3(c)
+                tb(r)
+            if r == 0:
+                uf_fill()
+            for g in range(NT // BG):
+                if max(BG * g - 1, 0) == r:
+                    bt_fill(g)
+            if ok(r):
+                tw(r)

@@ -214,12 +214,10 @@ def tile_generictreelstmcell_t_kernel(
             z_ps[t] = banks
 
         def sg(t):
-            zb = z_pool.tile([P, 4, H, 2], F32, name="zb")
+            zb = z_pool.tile([P, D, H], F32, name="zb")
             for k in range(2):
                 nc.scalar.activation(
-                    out=zb[:, 2 * k : 2 * k + 2, :, :],
-                    in_=z_ps[t][k][:].rearrange("p (q e) o -> p q o e", e=2),
-                    func=ACT.Sigmoid,
+                    out=zb[:, 4 * k : 4 * k + 4, :], in_=z_ps[t][k][:], func=ACT.Sigmoid
                 )
             zb_sb[t] = zb
 
@@ -229,19 +227,23 @@ def tile_generictreelstmcell_t_kernel(
             nc.vector.tensor_tensor(
                 out=zb[:],
                 in0=zb[:],
-                in1=c_tiles[c][:, tt, :].rearrange("p (q e o) -> p q o e", e=2, o=H),
+                in1=c_tiles[c][:, tt, :].rearrange("p (d o) -> p d o", o=H),
                 op=ALU.mult,
             )
 
-        def rd(t):
+        def add_halves(t, n):
+            zb = zb_sb[t]
+            nc.vector.tensor_tensor(
+                out=zb[:, 0:n, :], in0=zb[:, 0:n, :], in1=zb[:, n : 2 * n, :], op=ALU.add
+            )
+
+        def add_last(t):
             c, tt = divmod(t, CH)
+            zb = zb_sb[t]
             if tt == 0:
                 ca_sb[c] = fin.tile([P, CH, H], F32, name="ca")
-            nc.vector.tensor_reduce(
-                out=ca_sb[c][:, tt, :],
-                in_=zb_sb[t][:].rearrange("p q o e -> p o q e"),
-                axis=AX.XY,
-                op=ALU.add,
+            nc.vector.tensor_tensor(
+                out=ca_sb[c][:, tt, :], in0=zb[:, 0, :], in1=zb[:, 1, :], op=ALU.add
             )
 
         def mx(t):
@@ -383,19 +385,24 @@ def tile_generictreelstmcell_t_kernel(
                     w_evac(i)
             if ok(r - 4):
                 mu(r - 4)
+            if ok(r - 5):
+                add_halves(r - 5, 4)
             for t in late(r, 1):
                 st(t)
+            if ok(r - 5):
+                add_halves(r - 5, 2)
             if ok(r - 2):
                 qx(r - 2)
             if r == W_READY:
                 w_quant()
+            if ok(r - 5):
+                add_last(r - 5)
             for t in late(r, 3):
                 f1(t)
-                f2(t)
             for t in late(r, 5):
                 f3(t)
-            if ok(r - 5):
-                rd(r - 5)
+            for t in late(r, 3):
+                f2(t)
             if ok(r - 2):
                 fm(r - 2)
             for t in late(r, 0):

@@ -21,7 +21,10 @@ CH = 4
 NCH = NT // CH
 COLS = ((0, 256), (256, 384))
 BG = 4
-W_READY = 4
+W_READY = 3
+EW_HEAD = 0
+GROUPS = (1, 1) + (2,) * 15
+ENDS = (4,) * 7 + (2, 1, 1)
 
 FLOPS = 2 * N_NODES * D * H * 3 * H + 2 * N_NODES * D * H * H
 
@@ -43,9 +46,9 @@ def tile_generictreelstmcell_t_kernel(
         c_pool = ctx.enter_context(tc.tile_pool(name="cin", bufs=3))
         xt_pool = ctx.enter_context(tc.tile_pool(name="xts", bufs=3))
         g_pool = ctx.enter_context(tc.tile_pool(name="grp", bufs=3))
-        q_pool = ctx.enter_context(tc.tile_pool(name="quant", bufs=10))
+        q_pool = ctx.enter_context(tc.tile_pool(name="quant", bufs=4))
         z_pool = ctx.enter_context(tc.tile_pool(name="zb", bufs=4))
-        fin = ctx.enter_context(tc.tile_pool(name="fin", bufs=4))
+        fin = ctx.enter_context(tc.tile_pool(name="fin", bufs=3))
         psum = ctx.enter_context(tc.psum_pool(name="psum", bufs=8))
         ctx.enter_context(tc.manual_schedule())
 
@@ -103,14 +106,14 @@ def tile_generictreelstmcell_t_kernel(
         load_nh(0, 0, 1)
         nc.sync.dma_start(out=ufs[:], in_=U_f.rearrange("d o h -> o d h"))
         nc.sync.dma_start(out=b_all[:, 0:CH, :], in_=b_v[:, 0:CH, :])
-        load_nh(0, 1, 2)
-        alloc_c(0)
-        load_c(0, 0, 1)
         for jb in range(3):
             nc.sync.dma_start(
                 out=uis[:, jb, :].rearrange("p (d h) -> p d h", d=D),
                 in_=U_iou[:, jb * P : (jb + 1) * P, :].rearrange("d j h -> j d h"),
             )
+        load_nh(0, 1, 2)
+        alloc_c(0)
+        load_c(0, 0, 1)
         load_nh(0, 2, CH)
         load_c(0, 1, CH)
         nc.sync.dma_start(out=iou_all[:, 0:8, :], in_=iou_v[:, 0:8, :])
@@ -132,6 +135,19 @@ def tile_generictreelstmcell_t_kernel(
 
         def ok(t):
             return 0 <= t < NT
+
+        def ew_on_vector(t):
+            return t < EW_HEAD
+
+        def spans(sizes):
+            out = []
+            for n in sizes:
+                out.append((sum(x[1] for x in out), n))
+            return out
+
+        groups = spans(GROUPS)
+        ends = spans(ENDS)
+        grp_of = [g for g in range(len(groups)) for i in range(groups[g][1])]
 
         def uf_fill():
             uf_ps = bank([P, D, H], BF16)
@@ -171,20 +187,27 @@ def tile_generictreelstmcell_t_kernel(
             wt_ps[t] = wt
 
         def ew(t):
-            gq = g_pool.tile([P, 512], F32, name="gq", align_bytes=64)
-            nc.scalar.copy(
-                out=gq[:].rearrange("p (g n u) -> p g n u", g=2, u=2),
-                in_=wt_ps[t][:].rearrange("p (g u) n -> p g n u", u=2),
-            )
-            gq_sb[t] = gq
+            g = grp_of[t]
+            t0, n = groups[g]
+            if t == t0:
+                gq_sb[g] = g_pool.tile([P, n, 512], F32, name="gq", align_bytes=64)
+            dst = gq_sb[g][:, t - t0, :].rearrange("p (g n u) -> p g n u", g=2, u=2)
+            words = wt_ps[t][:].rearrange("p (g u) n -> p g n u", u=2)
+            if ew_on_vector(t):
+                nc.vector.tensor_copy(out=dst, in_=words)
+            else:
+                nc.scalar.copy(out=dst, in_=words)
 
-        def qx(t):
-            codes = q_pool.tile([P, 256], U32, name="codes", align_bytes=64)
-            scales = q_pool.tile([P, 256], U8, name="scales", align_bytes=64)
+        def qx(g):
+            t0, n = groups[g]
+            codes = q_pool.tile([P, n * 256], U32, name="codes", align_bytes=64)
+            scales = q_pool.tile([P, n * 256], U8, name="scales", align_bytes=64)
             nc.vector.quantize_mx(
-                out=codes[:].bitcast(FP8X4), scales=scales[:], in_=gq_sb[t][:].bitcast(BF16)
+                out=codes[:].bitcast(FP8X4),
+                scales=scales[:],
+                in_=gq_sb[g][:].rearrange("p n w -> p (n w)").bitcast(BF16),
             )
-            code_sb[t] = (codes, scales)
+            code_sb[g] = (codes, scales)
 
         def fm(t):
             xT = xT_sb[t]
@@ -214,51 +237,57 @@ def tile_generictreelstmcell_t_kernel(
             z_ps[t] = banks
 
         def sg(t):
-            zb = z_pool.tile([P, D, H], F32, name="zb")
+            g = grp_of[t]
+            t0, n = groups[g]
+            if t == t0:
+                zb_sb[g] = z_pool.tile([P, n, D, H], F32, name="zb")
             for k in range(2):
                 nc.scalar.activation(
-                    out=zb[:, 4 * k : 4 * k + 4, :], in_=z_ps[t][k][:], func=ACT.Sigmoid
+                    out=zb_sb[g][:, t - t0, 4 * k : 4 * k + 4, :], in_=z_ps[t][k][:], func=ACT.Sigmoid
                 )
-            zb_sb[t] = zb
 
-        def mu(t):
-            c, tt = divmod(t, CH)
-            zb = zb_sb[t]
+        def mu(g):
+            t0, n = groups[g]
+            c, tt = divmod(t0, CH)
+            zb = zb_sb[g]
             nc.vector.tensor_tensor(
                 out=zb[:],
                 in0=zb[:],
-                in1=c_tiles[c][:, tt, :].rearrange("p (d o) -> p d o", o=H),
+                in1=c_tiles[c][:, tt : tt + n, :].rearrange("p n (d o) -> p n d o", o=H),
                 op=ALU.mult,
             )
 
-        def add_halves(t, n):
-            zb = zb_sb[t]
+        def add_halves(g, m):
+            zb = zb_sb[g]
             nc.vector.tensor_tensor(
-                out=zb[:, 0:n, :], in0=zb[:, 0:n, :], in1=zb[:, n : 2 * n, :], op=ALU.add
+                out=zb[:, :, 0:m, :], in0=zb[:, :, 0:m, :], in1=zb[:, :, m : 2 * m, :], op=ALU.add
             )
 
-        def add_last(t):
-            c, tt = divmod(t, CH)
-            zb = zb_sb[t]
+        def add_last(g):
+            t0, n = groups[g]
+            c, tt = divmod(t0, CH)
+            zb = zb_sb[g]
             if tt == 0:
                 ca_sb[c] = fin.tile([P, CH, H], F32, name="ca")
             nc.vector.tensor_tensor(
-                out=ca_sb[c][:, tt, :], in0=zb[:, 0, :], in1=zb[:, 1, :], op=ALU.add
+                out=ca_sb[c][:, tt : tt + n, :], in0=zb[:, :, 0, :], in1=zb[:, :, 1, :], op=ALU.add
             )
 
         def mx(t):
-            codes, scales = code_sb[t]
+            g = grp_of[t]
+            codes, scales = code_sb[g]
+            base = (t - groups[g][0]) * 256
             acc = bank([P, 3 * H], F32)
             for j0, j1 in COLS:
-                for g in range(2):
+                for s in range(2):
                     nc.tensor.matmul_mx(
                         out=acc[:, j0:j1],
-                        lhsT=codes[:, g * P : (g + 1) * P].bitcast(FP8X4),
-                        lhsT_scale=scales[:, g * P : (g + 1) * P],
-                        rhs=wcodes[:, g, j0:j1].bitcast(FP8X4),
-                        rhs_scale=wscales[:, g, j0:j1],
-                        start=(g == 0),
-                        stop=(g == 1),
+                        lhsT=codes[:, base + s * P : base + (s + 1) * P].bitcast(FP8X4),
+                        lhsT_scale=scales[:, base + s * P : base + (s + 1) * P],
+                        rhs=wcodes[:, s, j0:j1].bitcast(FP8X4),
+                        rhs_scale=wscales[:, s, j0:j1],
+                        start=(s == 0),
+                        stop=(s == 1),
                     )
             acc_ps[t] = acc
 
@@ -289,7 +318,7 @@ def tile_generictreelstmcell_t_kernel(
             wf_ps[i] = wf
 
         def w_evac(i):
-            nc.scalar.copy(
+            nc.vector.tensor_copy(
                 out=wg[:, 2 * i : 2 * i + 2, :, :],
                 in_=wf_ps[i][:].rearrange("p c u j -> p c j u"),
             )
@@ -304,62 +333,74 @@ def tile_generictreelstmcell_t_kernel(
                         in_=wflat[:, g, 2 * j0 : 2 * j1].bitcast(BF16),
                     )
 
-        def fa(t):
-            c, tt = divmod(t, CH)
-            s = iou_sb[c]
+        def fa(e):
+            t0, n = ends[e]
+            c, tt = divmod(t0, CH)
+            s = iou_sb[c][:, tt : tt + n, :]
+            nc.scalar.activation(out=s[:, :, 0 : 2 * H], in_=s[:, :, 0 : 2 * H], func=ACT.Sigmoid)
             nc.scalar.activation(
-                out=s[:, tt, 0 : 2 * H], in_=s[:, tt, 0 : 2 * H], func=ACT.Sigmoid
-            )
-            nc.scalar.activation(
-                out=s[:, tt, 2 * H : 3 * H], in_=s[:, tt, 2 * H : 3 * H], func=ACT.Tanh
+                out=s[:, :, 2 * H : 3 * H], in_=s[:, :, 2 * H : 3 * H], func=ACT.Tanh
             )
 
-        def f1(t):
-            c, tt = divmod(t, CH)
-            s = iou_sb[c]
+        def f1(e):
+            t0, n = ends[e]
+            c, tt = divmod(t0, CH)
+            s = iou_sb[c][:, tt : tt + n, :]
             if tt == 0:
                 iu_sb[c] = fin.tile([P, CH, H], F32, name="iu")
             nc.vector.tensor_tensor(
-                out=iu_sb[c][:, tt, :], in0=s[:, tt, 0:H], in1=s[:, tt, 2 * H : 3 * H], op=ALU.mult
+                out=iu_sb[c][:, tt : tt + n, :], in0=s[:, :, 0:H], in1=s[:, :, 2 * H : 3 * H], op=ALU.mult
             )
 
-        def f2(t):
-            c, tt = divmod(t, CH)
+        def f2(e):
+            t0, n = ends[e]
+            c, tt = divmod(t0, CH)
             if tt == 0:
                 c_sb[c] = fin.tile([P, CH, H], F32, name="c_o")
             nc.vector.tensor_tensor(
-                out=c_sb[c][:, tt, :], in0=iu_sb[c][:, tt, :], in1=ca_sb[c][:, tt, :], op=ALU.add
+                out=c_sb[c][:, tt : tt + n, :],
+                in0=iu_sb[c][:, tt : tt + n, :],
+                in1=ca_sb[c][:, tt : tt + n, :],
+                op=ALU.add,
             )
-            if tt == CH - 1:
-                nc.sync.dma_start(out=c_out_v[:, c * CH : (c + 1) * CH, :], in_=c_sb[c][:])
+            nc.sync.dma_start(out=c_out_v[:, t0 : t0 + n, :], in_=c_sb[c][:, tt : tt + n, :])
 
-        def fb(t):
-            c, tt = divmod(t, CH)
+        def fb(e):
+            t0, n = ends[e]
+            c, tt = divmod(t0, CH)
             if tt == 0:
                 tch_sb[c] = fin.tile([P, CH, H], F32, name="tch")
-            nc.scalar.activation(out=tch_sb[c][:, tt, :], in_=c_sb[c][:, tt, :], func=ACT.Tanh)
+            nc.scalar.activation(
+                out=tch_sb[c][:, tt : tt + n, :], in_=c_sb[c][:, tt : tt + n, :], func=ACT.Tanh
+            )
 
-        def f3(t):
-            c, tt = divmod(t, CH)
+        def f3(e):
+            t0, n = ends[e]
+            c, tt = divmod(t0, CH)
             if tt == 0:
                 h_sb[c] = fin.tile([P, CH, H], F32, name="h_o")
             nc.vector.tensor_tensor(
-                out=h_sb[c][:, tt, :], in0=iou_sb[c][:, tt, H : 2 * H], in1=tch_sb[c][:, tt, :], op=ALU.mult
+                out=h_sb[c][:, tt : tt + n, :],
+                in0=iou_sb[c][:, tt : tt + n, H : 2 * H],
+                in1=tch_sb[c][:, tt : tt + n, :],
+                op=ALU.mult,
             )
-            if tt == CH - 1:
-                nc.sync.dma_start(out=h_out_v[:, c * CH : (c + 1) * CH, :], in_=h_sb[c][:])
+            nc.sync.dma_start(out=h_out_v[:, t0 : t0 + n, :], in_=h_sb[c][:, tt : tt + n, :])
 
-        def m_round(t):
-            return max(t + 3, W_READY + 1 + t // 2)
+        r_qx = [t0 + n - 1 + 2 for t0, n in groups]
+        r_mu = [t0 + n - 1 + 4 for t0, n in groups]
+        r_a1 = [r_mu[g + 1] if g + 1 < len(groups) else r_mu[g] + 1 for g in range(len(groups))]
+        r_a2 = [x + 1 for x in r_a1]
+        r_mx = [
+            max(r_qx[grp_of[t]] + 1 + t - groups[grp_of[t]][0], W_READY + 1 + t // 2) for t in range(NT)
+        ]
+        r_fa = [max(r_mx[t] for t in range(t0, t0 + n)) + 2 for t0, n in ends]
+        r_f2 = [max(r_fa[e] + 1, r_a2[grp_of[ends[e][0] + ends[e][1] - 1]] + 1) for e in range(len(ends))]
 
-        by_round = {}
-        for t in range(NT):
-            by_round.setdefault(m_round(t), []).append(t)
+        def due(rounds, r):
+            return [i for i in range(len(rounds)) if rounds[i] == r]
 
-        def late(r, k):
-            return by_round.get(r - k, [])
-
-        for r in range(0, m_round(NT - 1) + 6):
+        for r in range(0, max(r_f2) + 3):
             if r >= 5 and (r - 5) % CH == 0:
                 m = (r - 5) // CH
                 if m + 3 < NCH:
@@ -370,42 +411,45 @@ def tile_generictreelstmcell_t_kernel(
                     load_c(m + 2, 0, CH)
             if ok(r - 3):
                 sg(r - 3)
-            for t in late(r, 2):
-                fa(t)
-            for t in late(r, 4):
-                fb(t)
+            for e in due(r_fa, r):
+                fa(e)
+            for e in due(r_f2, r - 1):
+                fb(e)
             if ok(r - 1):
                 ex(r - 1)
+            if ok(r - 1) and not ew_on_vector(r - 1):
                 ew(r - 1)
             for g in range(NT // BG):
-                if max(BG * g, 1) == r:
+                if BG * g + 1 == r:
                     bt_evac(g)
+            if ok(r - 1) and ew_on_vector(r - 1):
+                ew(r - 1)
             if r == W_READY - 1:
                 for i in range(3):
                     w_evac(i)
-            if ok(r - 4):
-                mu(r - 4)
-            if ok(r - 5):
-                add_halves(r - 5, 4)
-            for t in late(r, 1):
+            for g in due(r_a2, r):
+                add_halves(g, 2)
+            for t in due(r_mx, r - 1):
                 st(t)
-            if ok(r - 5):
-                add_halves(r - 5, 2)
-            if ok(r - 2):
-                qx(r - 2)
+            for g in due(r_a2, r):
+                add_last(g)
+            for g in due(r_mu, r):
+                mu(g)
+            for g in due(r_a1, r):
+                add_halves(g, 4)
+            for g in due(r_qx, r):
+                qx(g)
             if r == W_READY:
                 w_quant()
-            if ok(r - 5):
-                add_last(r - 5)
-            for t in late(r, 3):
-                f1(t)
-            for t in late(r, 5):
-                f3(t)
-            for t in late(r, 3):
-                f2(t)
+            for e in due(r_fa, r - 1):
+                f1(e)
+            for e in due(r_f2, r - 2):
+                f3(e)
+            for e in due(r_f2, r):
+                f2(e)
             if ok(r - 2):
                 fm(r - 2)
-            for t in late(r, 0):
+            for t in due(r_mx, r):
                 mx(t)
             if r == W_READY - 2:
                 for i in range(3):
@@ -415,7 +459,7 @@ def tile_generictreelstmcell_t_kernel(
             if r == 0:
                 uf_fill()
             for g in range(NT // BG):
-                if max(BG * g - 1, 0) == r:
+                if BG * g == r:
                     bt_fill(g)
             if ok(r):
                 tw(r)

@@ -22,8 +22,7 @@ NCH = NT // CH
 COLS = ((0, 256), (256, 384))
 BG = 4
 W_READY = 3
-EW_HEAD = 0
-GROUPS = (1, 1) + (2,) * 15
+GROUPS = (1,) * 32
 ENDS = (4,) * 7 + (2, 1, 1)
 
 FLOPS = 2 * N_NODES * D * H * 3 * H + 2 * N_NODES * D * H * H
@@ -44,7 +43,6 @@ def tile_generictreelstmcell_t_kernel(
         const = ctx.enter_context(tc.tile_pool(name="const", bufs=1))
         nh_pool = ctx.enter_context(tc.tile_pool(name="nh", bufs=3))
         c_pool = ctx.enter_context(tc.tile_pool(name="cin", bufs=3))
-        xt_pool = ctx.enter_context(tc.tile_pool(name="xts", bufs=3))
         g_pool = ctx.enter_context(tc.tile_pool(name="grp", bufs=3))
         q_pool = ctx.enter_context(tc.tile_pool(name="quant", bufs=4))
         z_pool = ctx.enter_context(tc.tile_pool(name="zb", bufs=4))
@@ -58,9 +56,7 @@ def tile_generictreelstmcell_t_kernel(
         nh_tiles = {}
         c_tiles = {}
         xt_ps = {}
-        xT_sb = {}
-        wt_ps = {}
-        gq_sb = {}
+        gx_sb = {}
         code_sb = {}
         z_ps = {}
         zb_sb = {}
@@ -129,15 +125,12 @@ def tile_generictreelstmcell_t_kernel(
 
         ufT = const.tile([P, D, H], BF16)
         bT = const.tile([P, NT, P], F32)
-        wg = const.tile([P, 6, P, 2], F32, align_bytes=64)
+        wg = const.tile([P, 2, 3 * H, 4], BF16, align_bytes=64)
         wcodes = const.tile([P, 2, 3 * H], U32, align_bytes=64)
         wscales = const.tile([P, 2, 3 * H], U8, align_bytes=64)
 
         def ok(t):
             return 0 <= t < NT
-
-        def ew_on_vector(t):
-            return t < EW_HEAD
 
         def spans(sizes):
             out = []
@@ -174,29 +167,14 @@ def tile_generictreelstmcell_t_kernel(
             xt_ps[t] = xt
 
         def ex(t):
-            xT = xt_pool.tile([P, D, P], BF16, name="xT")
-            nc.scalar.copy(out=xT[:], in_=xt_ps[t][:])
-            xT_sb[t] = xT
-
-        def tw(t):
-            c, tt = divmod(t, CH)
-            wt = bank([P, 4, P], F32)
-            words = nh_tiles[c][:, tt, :].bitcast(F32)
-            for s in range(4):
-                nc.tensor.transpose(wt[:, s, :], words[:, s * P : (s + 1) * P], ident_f[:])
-            wt_ps[t] = wt
-
-        def ew(t):
             g = grp_of[t]
             t0, n = groups[g]
             if t == t0:
-                gq_sb[g] = g_pool.tile([P, n, 512], F32, name="gq", align_bytes=64)
-            dst = gq_sb[g][:, t - t0, :].rearrange("p (g n u) -> p g n u", g=2, u=2)
-            words = wt_ps[t][:].rearrange("p (g u) n -> p g n u", u=2)
-            if ew_on_vector(t):
-                nc.vector.tensor_copy(out=dst, in_=words)
-            else:
-                nc.scalar.copy(out=dst, in_=words)
+                gx_sb[g] = g_pool.tile([P, n, 2, P, 4], BF16, name="gx", align_bytes=64)
+            nc.scalar.copy(
+                out=gx_sb[g][:, t - t0, :, :, :],
+                in_=xt_ps[t][:].rearrange("p (s j) n -> p s n j", j=4),
+            )
 
         def qx(g):
             t0, n = groups[g]
@@ -205,12 +183,13 @@ def tile_generictreelstmcell_t_kernel(
             nc.vector.quantize_mx(
                 out=codes[:].bitcast(FP8X4),
                 scales=scales[:],
-                in_=gq_sb[g][:].rearrange("p n w -> p (n w)").bitcast(BF16),
+                in_=gx_sb[g][:].rearrange("p n s m j -> p (n s m j)"),
             )
             code_sb[g] = (codes, scales)
 
         def fm(t):
-            xT = xT_sb[t]
+            g = grp_of[t]
+            gx = gx_sb[g][:, t - groups[g][0], :, :, :]
             banks = []
             for k in range(2):
                 z = bank([P, 4, H], F32)
@@ -229,7 +208,7 @@ def tile_generictreelstmcell_t_kernel(
                     d = 4 * k + j
                     nc.tensor.matmul(
                         banks[k][:, j, :],
-                        lhsT=xT[:, d, :],
+                        lhsT=gx[:, k, :, j],
                         rhs=ufT[:, d, :],
                         start=False,
                         stop=(j == 3),
@@ -304,33 +283,25 @@ def tile_generictreelstmcell_t_kernel(
                 op1=ALU.add,
             )
 
-        def w_fill(i):
-            wf = bank([P, 2, 2, P], F32)
-            for cb in range(2):
-                g, jb = divmod(2 * i + cb, 3)
-                for u in range(2):
-                    s = 2 * g + u
-                    nc.tensor.transpose(
-                        wf[:, cb, u, :],
-                        uis[:, jb, :].bitcast(F32)[:, s * P : (s + 1) * P],
-                        ident_f[:],
-                    )
-            wf_ps[i] = wf
+        def w_fill(jb):
+            wf = bank([P, D, P], BF16)
+            for d in range(D):
+                nc.tensor.transpose(wf[:, d, :], uis[:, jb, d * H : (d + 1) * H], ident_b[:])
+            wf_ps[jb] = wf
 
-        def w_evac(i):
+        def w_evac(jb):
             nc.vector.tensor_copy(
-                out=wg[:, 2 * i : 2 * i + 2, :, :],
-                in_=wf_ps[i][:].rearrange("p c u j -> p c j u"),
+                out=wg[:, :, jb * P : (jb + 1) * P, :],
+                in_=wf_ps[jb][:].rearrange("p (s j) m -> p s m j", j=4),
             )
 
         def w_quant():
-            wflat = wg[:].rearrange("p (g b) j u -> p g (b j u)", g=2)
-            for g in range(2):
+            for s in range(2):
                 for j0, j1 in COLS:
                     nc.vector.quantize_mx(
-                        out=wcodes[:, g, j0:j1].bitcast(FP8X4),
-                        scales=wscales[:, g, j0:j1],
-                        in_=wflat[:, g, 2 * j0 : 2 * j1].bitcast(BF16),
+                        out=wcodes[:, s, j0:j1].bitcast(FP8X4),
+                        scales=wscales[:, s, j0:j1],
+                        in_=wg[:, s, j0:j1, :].rearrange("p m j -> p (m j)"),
                     )
 
         def fa(e):
@@ -417,13 +388,9 @@ def tile_generictreelstmcell_t_kernel(
                 fb(e)
             if ok(r - 1):
                 ex(r - 1)
-            if ok(r - 1) and not ew_on_vector(r - 1):
-                ew(r - 1)
             for g in range(NT // BG):
                 if BG * g + 1 == r:
                     bt_evac(g)
-            if ok(r - 1) and ew_on_vector(r - 1):
-                ew(r - 1)
             if r == W_READY - 1:
                 for i in range(3):
                     w_evac(i)
@@ -461,5 +428,3 @@ def tile_generictreelstmcell_t_kernel(
             for g in range(NT // BG):
                 if BG * g == r:
                     bt_fill(g)
-            if ok(r):
-                tw(r)

@@ -24,6 +24,7 @@ BG = 4
 W_READY = 3
 GROUPS = (1,) * 32
 ENDS = (4,) * 7 + (2, 1, 1)
+PE_SUM = (4, 2, 30)
 
 FLOPS = 2 * N_NODES * D * H * 3 * H + 2 * N_NODES * D * H * H
 
@@ -46,6 +47,7 @@ def tile_generictreelstmcell_t_kernel(
         g_pool = ctx.enter_context(tc.tile_pool(name="grp", bufs=3))
         q_pool = ctx.enter_context(tc.tile_pool(name="quant", bufs=4))
         z_pool = ctx.enter_context(tc.tile_pool(name="zb", bufs=4))
+        t_pool = ctx.enter_context(tc.tile_pool(name="caT", bufs=2))
         fin = ctx.enter_context(tc.tile_pool(name="fin", bufs=3))
         psum = ctx.enter_context(tc.psum_pool(name="psum", bufs=8))
         ctx.enter_context(tc.manual_schedule())
@@ -69,6 +71,9 @@ def tile_generictreelstmcell_t_kernel(
         h_sb = {}
         wf_ps = {}
         bt_ps = {}
+        caT_ps = {}
+        caT_sb = {}
+        ca_ps = {}
 
         def alloc_nh(c):
             nh_tiles[c] = nh_pool.tile([P, CH, D * H], BF16, name="nh_sb")
@@ -242,12 +247,51 @@ def tile_generictreelstmcell_t_kernel(
                 out=zb[:, :, 0:m, :], in0=zb[:, :, 0:m, :], in1=zb[:, :, m : 2 * m, :], op=ALU.add
             )
 
+        def ca_of(c):
+            if c not in ca_sb:
+                ca_sb[c] = fin.tile([P, CH, H], F32, name="ca")
+            return ca_sb[c]
+
+        def on_pe(g):
+            return g % PE_SUM[0] == PE_SUM[1] and g < PE_SUM[2]
+
+        def sum_fill(g):
+            t0, n = groups[g]
+            ps = bank([P, n, P], F32)
+            for i in range(n):
+                for d in range(D):
+                    nc.tensor.matmul(
+                        ps[:, i, :],
+                        lhsT=zb_sb[g][:, i, d, :],
+                        rhs=ident_f[:],
+                        start=(d == 0),
+                        stop=(d == D - 1),
+                        is_transpose=True,
+                    )
+            caT_ps[g] = ps
+
+        def sum_evac(g):
+            t0, n = groups[g]
+            caT_sb[g] = t_pool.tile([P, n, P], F32, name="caT")
+            nc.scalar.copy(out=caT_sb[g][:], in_=caT_ps[g][:])
+
+        def sum_back(g):
+            t0, n = groups[g]
+            ps = bank([P, n, P], F32)
+            for i in range(n):
+                nc.tensor.transpose(ps[:, i, :], caT_sb[g][:, i, :], ident_f[:])
+            ca_ps[g] = ps
+
+        def sum_out(g):
+            t0, n = groups[g]
+            c, tt = divmod(t0, CH)
+            nc.scalar.copy(out=ca_of(c)[:, tt : tt + n, :], in_=ca_ps[g][:])
+
         def add_last(g):
             t0, n = groups[g]
             c, tt = divmod(t0, CH)
             zb = zb_sb[g]
-            if tt == 0:
-                ca_sb[c] = fin.tile([P, CH, H], F32, name="ca")
+            ca_of(c)
             nc.vector.tensor_tensor(
                 out=ca_sb[c][:, tt : tt + n, :], in0=zb[:, :, 0, :], in1=zb[:, :, 1, :], op=ALU.add
             )
@@ -362,11 +406,21 @@ def tile_generictreelstmcell_t_kernel(
         r_mu = [t0 + n - 1 + 4 for t0, n in groups]
         r_a1 = [r_mu[g + 1] if g + 1 < len(groups) else r_mu[g] + 1 for g in range(len(groups))]
         r_a2 = [x + 1 for x in r_a1]
+        NEVER = -99
+        r_sf = [r_mu[g] + 1 if on_pe(g) else NEVER for g in range(len(groups))]
+        r_ca = [r_sf[g] + 3 if on_pe(g) else r_a2[g] for g in range(len(groups))]
+        for g in range(len(groups)):
+            if on_pe(g):
+                r_a1[g] = NEVER
+                r_a2[g] = NEVER
         r_mx = [
             max(r_qx[grp_of[t]] + 1 + t - groups[grp_of[t]][0], W_READY + 1 + t // 2) for t in range(NT)
         ]
         r_fa = [max(r_mx[t] for t in range(t0, t0 + n)) + 2 for t0, n in ends]
-        r_f2 = [max(r_fa[e] + 1, r_a2[grp_of[ends[e][0] + ends[e][1] - 1]] + 1) for e in range(len(ends))]
+        r_f2 = [
+            max(r_fa[e] + 1, max(r_ca[grp_of[t]] for t in range(ends[e][0], ends[e][0] + ends[e][1])) + 1)
+            for e in range(len(ends))
+        ]
 
         def due(rounds, r):
             return [i for i in range(len(rounds)) if rounds[i] == r]
@@ -386,6 +440,10 @@ def tile_generictreelstmcell_t_kernel(
                 fa(e)
             for e in due(r_f2, r - 1):
                 fb(e)
+            for g in due(r_sf, r - 1):
+                sum_evac(g)
+            for g in due(r_sf, r - 3):
+                sum_out(g)
             if ok(r - 1):
                 ex(r - 1)
             for g in range(NT // BG):
@@ -418,6 +476,10 @@ def tile_generictreelstmcell_t_kernel(
                 fm(r - 2)
             for t in due(r_mx, r):
                 mx(t)
+            for g in due(r_sf, r):
+                sum_fill(g)
+            for g in due(r_sf, r - 2):
+                sum_back(g)
             if r == W_READY - 2:
                 for i in range(3):
                     w_fill(i)

@@ -24,7 +24,7 @@ BG = 4
 W_READY = 3
 GROUPS = (1,) * 32
 ENDS = (4,) * 7 + (2, 1, 1)
-PE_SUM = (4, 2, 30)
+PE_EVERY, PE_REST, PE_TAIL, PE_END = 4, 2, 25, 31
 
 FLOPS = 2 * N_NODES * D * H * 3 * H + 2 * N_NODES * D * H * H
 
@@ -253,7 +253,7 @@ def tile_generictreelstmcell_t_kernel(
             return ca_sb[c]
 
         def on_pe(g):
-            return g % PE_SUM[0] == PE_SUM[1] and g < PE_SUM[2]
+            return g < PE_END and (g % PE_EVERY == PE_REST or g >= PE_TAIL)
 
         def sum_fill(g):
             t0, n = groups[g]

@@ -413,9 +413,7 @@ def tile_generictreelstmcell_t_kernel(
             if on_pe(g):
                 r_a1[g] = NEVER
                 r_a2[g] = NEVER
-        r_mx = [
-            max(r_qx[grp_of[t]] + 1 + t - groups[grp_of[t]][0], W_READY + 1 + t // 2) for t in range(NT)
-        ]
+        r_mx = [max(r_qx[t | 1] + 1, W_READY + 1) for t in range(NT)]
         r_fa = [max(r_mx[t] for t in range(t0, t0 + n)) + 2 for t0, n in ends]
         r_f2 = [
             max(r_fa[e] + 1, max(r_ca[grp_of[t]] for t in range(ends[e][0], ends[e][0] + ends[e][1])) + 1)
@@ -454,14 +452,14 @@ def tile_generictreelstmcell_t_kernel(
                     w_evac(i)
             for g in due(r_a2, r):
                 add_halves(g, 2)
-            for t in due(r_mx, r - 1):
-                st(t)
-            for g in due(r_a2, r):
-                add_last(g)
             for g in due(r_mu, r):
                 mu(g)
+            for g in due(r_a2, r):
+                add_last(g)
             for g in due(r_a1, r):
                 add_halves(g, 4)
+            for t in due(r_mx, r - 1):
+                st(t)
             for g in due(r_qx, r):
                 qx(g)
             if r == W_READY:

@@ -24,7 +24,7 @@ BG = 4
 W_READY = 3
 GROUPS = (1,) * 32
 ENDS = (4,) * 7 + (2, 1, 1)
-PE_EVERY, PE_REST, PE_TAIL, PE_END = 4, 2, 25, 31
+PE_EVERY, PE_REST, PE_TAIL, PE_END = 4, 2, 27, 31
 
 FLOPS = 2 * N_NODES * D * H * 3 * H + 2 * N_NODES * D * H * H
 

from contextlib import ExitStack

import concourse.mybir as mybir
from concourse.masks import make_identity

F32 = mybir.dt.float32
BF16 = mybir.dt.bfloat16
U32 = mybir.dt.uint32
U8 = mybir.dt.uint8
FP8X4 = mybir.dt.float8_e4m3fn_x4
ALU = mybir.AluOpType
ACT = mybir.ActivationFunctionType
AX = mybir.AxisListType

P = 128
N_NODES = 4096
D = 8
H = 128
NT = N_NODES // P
CH = 4
NCH = NT // CH
COLS = ((0, 256), (256, 384))
BG = 4
W_READY = 3
GROUPS = (1,) * 32
ENDS = (4,) * 7 + (2, 1, 1)
PE_EVERY, PE_REST, PE_TAIL, PE_END = 4, 2, 27, 31

FLOPS = 2 * N_NODES * D * H * 3 * H + 2 * N_NODES * D * H * H


def tile_generictreelstmcell_t_kernel(
    tc, neighbour_h, neighbour_c, f_input, iou_input, U_f, U_iou, out_0, out_1
):
    nc = tc.nc
    nh_v = neighbour_h.rearrange("(p t) d h -> p t (d h)", t=NT)
    c_v = neighbour_c.rearrange("(p t) d h -> p t (d h)", t=NT)
    b_v = f_input.rearrange("(p t) o -> p t o", t=NT)
    iou_v = iou_input.rearrange("(p t) j -> p t j", t=NT)
    h_out_v = out_0.rearrange("(p t) o -> p t o", t=NT)
    c_out_v = out_1.rearrange("(p t) o -> p t o", t=NT)

    with ExitStack() as ctx:
        const = ctx.enter_context(tc.tile_pool(name="const", bufs=1))
        nh_pool = ctx.enter_context(tc.tile_pool(name="nh", bufs=3))
        c_pool = ctx.enter_context(tc.tile_pool(name="cin", bufs=3))
        g_pool = ctx.enter_context(tc.tile_pool(name="grp", bufs=3))
        q_pool = ctx.enter_context(tc.tile_pool(name="quant", bufs=4))
        z_pool = ctx.enter_context(tc.tile_pool(name="zb", bufs=4))
        t_pool = ctx.enter_context(tc.tile_pool(name="caT", bufs=2))
        fin = ctx.enter_context(tc.tile_pool(name="fin", bufs=3))
        psum = ctx.enter_context(tc.psum_pool(name="psum", bufs=8))
        ctx.enter_context(tc.manual_schedule())

        def bank(shape, dtype):
            return psum.tile(shape, dtype, tag="ring", bufs=8, name="ring")

        nh_tiles = {}
        c_tiles = {}
        xt_ps = {}
        gx_sb = {}
        code_sb = {}
        z_ps = {}
        zb_sb = {}
        acc_ps = {}
        ca_sb = {}
        iou_sb = {}
        iu_sb = {}
        c_sb = {}
        tch_sb = {}
        h_sb = {}
        wf_ps = {}
        bt_ps = {}
        caT_ps = {}
        caT_sb = {}
        ca_ps = {}

        def alloc_nh(c):
            nh_tiles[c] = nh_pool.tile([P, CH, D * H], BF16, name="nh_sb")

        def load_nh(c, t0, t1):
            nc.sync.dma_start(
                out=nh_tiles[c][:, t0:t1, :], in_=nh_v[:, c * CH + t0 : c * CH + t1, :]
            )

        def alloc_c(c):
            c_tiles[c] = c_pool.tile([P, CH, D * H], BF16, name="c_in")

        def load_c(c, t0, t1):
            nc.sync.dma_start(
                out=c_tiles[c][:, t0:t1, :], in_=c_v[:, c * CH + t0 : c * CH + t1, :]
            )

        warm = const.tile([P, 1], F32)
        nc.vector.memset(warm[:], 0.0)
        nc.scalar.activation(out=warm[:], in_=warm[:], func=ACT.Sigmoid)
        ident_b = const.tile([P, P], BF16)
        make_identity(nc, ident_b[:])
        ident_f = const.tile([P, P], F32)
        make_identity(nc, ident_f[:])

        ufs = const.tile([P, D, H], BF16)
        uis = const.tile([P, 3, D * H], BF16)
        b_all = const.tile([P, NT, H], BF16)
        iou_all = const.tile([P, NT, 3 * H], BF16)
        alloc_nh(0)
        load_nh(0, 0, 1)
        nc.sync.dma_start(out=ufs[:], in_=U_f.rearrange("d o h -> o d h"))
        nc.sync.dma_start(out=b_all[:, 0:CH, :], in_=b_v[:, 0:CH, :])
        for jb in range(3):
            nc.sync.dma_start(
                out=uis[:, jb, :].rearrange("p (d h) -> p d h", d=D),
                in_=U_iou[:, jb * P : (jb + 1) * P, :].rearrange("d j h -> j d h"),
            )
        load_nh(0, 1, 2)
        alloc_c(0)
        load_c(0, 0, 1)
        load_nh(0, 2, CH)
        load_c(0, 1, CH)
        nc.sync.dma_start(out=iou_all[:, 0:8, :], in_=iou_v[:, 0:8, :])
        alloc_nh(1)
        load_nh(1, 0, CH)
        nc.sync.dma_start(out=b_all[:, 4:12, :], in_=b_v[:, 4:12, :])
        alloc_c(1)
        load_c(1, 0, CH)
        alloc_nh(2)
        load_nh(2, 0, CH)
        nc.sync.dma_start(out=b_all[:, 12:NT, :], in_=b_v[:, 12:NT, :])
        nc.sync.dma_start(out=iou_all[:, 8:NT, :], in_=iou_v[:, 8:NT, :])

        ufT = const.tile([P, D, H], BF16)
        bT = const.tile([P, NT, P], F32)
        wg = const.tile([P, 2, 3 * H, 4], BF16, align_bytes=64)
        wcodes = const.tile([P, 2, 3 * H], U32, align_bytes=64)
        wscales = const.tile([P, 2, 3 * H], U8, align_bytes=64)

        def ok(t):
            return 0 <= t < NT

        def spans(sizes):
            out = []
            for n in sizes:
                out.append((sum(x[1] for x in out), n))
            return out

        groups = spans(GROUPS)
        ends = spans(ENDS)
        grp_of = [g for g in range(len(groups)) for i in range(groups[g][1])]

        def uf_fill():
            uf_ps = bank([P, D, H], BF16)
            for d in range(D):
                nc.tensor.transpose(uf_ps[:, d, :], ufs[:, d, :], ident_b[:])
            nc.vector.tensor_copy(out=ufT[:], in_=uf_ps[:])

        def bt_fill(g):
            ps = bank([P, BG, P], BF16)
            for i in range(BG):
                nc.tensor.transpose(ps[:, i, :], b_all[:, BG * g + i, :], ident_b[:])
            bt_ps[g] = ps

        def bt_evac(g):
            nc.scalar.copy(out=bT[:, BG * g : BG * (g + 1), :], in_=bt_ps[g][:])

        def tb(t):
            c, tt = divmod(t, CH)
            xt = bank([P, D, P], BF16)
            for d in range(D):
                nc.tensor.transpose(
                    xt[:, d, :], nh_tiles[c][:, tt, d * H : (d + 1) * H], ident_b[:]
                )
            xt_ps[t] = xt

        def ex(t):
            g = grp_of[t]
            t0, n = groups[g]
            if t == t0:
                gx_sb[g] = g_pool.tile([P, n, 2, P, 4], BF16, name="gx", align_bytes=64)
            nc.scalar.copy(
                out=gx_sb[g][:, t - t0, :, :, :],
                in_=xt_ps[t][:].rearrange("p (s j) n -> p s n j", j=4),
            )

        def qx(g):
            t0, n = groups[g]
            codes = q_pool.tile([P, n * 256], U32, name="codes", align_bytes=64)
            scales = q_pool.tile([P, n * 256], U8, name="scales", align_bytes=64)
            nc.vector.quantize_mx(
                out=codes[:].bitcast(FP8X4),
                scales=scales[:],
                in_=gx_sb[g][:].rearrange("p n s m j -> p (n s m j)"),
            )
            code_sb[g] = (codes, scales)

        def fm(t):
            g = grp_of[t]
            gx = gx_sb[g][:, t - groups[g][0], :, :, :]
            banks = []
            for k in range(2):
                z = bank([P, 4, H], F32)
                for j in range(4):
                    nc.tensor.matmul(
                        z[:, j, :],
                        lhsT=bT[:, t, :],
                        rhs=ident_f[:],
                        start=(j == 0),
                        stop=False,
                        is_transpose=True,
                    )
                banks.append(z)
            for k in range(2):
                for j in range(4):
                    d = 4 * k + j
                    nc.tensor.matmul(
                        banks[k][:, j, :],
                        lhsT=gx[:, k, :, j],
                        rhs=ufT[:, d, :],
                        start=False,
                        stop=(j == 3),
                    )
            z_ps[t] = banks

        def sg(t):
            g = grp_of[t]
            t0, n = groups[g]
            if t == t0:
                zb_sb[g] = z_pool.tile([P, n, D, H], F32, name="zb")
            for k in range(2):
                nc.scalar.activation(
                    out=zb_sb[g][:, t - t0, 4 * k : 4 * k + 4, :], in_=z_ps[t][k][:], func=ACT.Sigmoid
                )

        def mu(g):
            t0, n = groups[g]
            c, tt = divmod(t0, CH)
            zb = zb_sb[g]
            nc.vector.tensor_tensor(
                out=zb[:],
                in0=zb[:],
                in1=c_tiles[c][:, tt : tt + n, :].rearrange("p n (d o) -> p n d o", o=H),
                op=ALU.mult,
            )

        def add_halves(g, m):
            zb = zb_sb[g]
            nc.vector.tensor_tensor(
                out=zb[:, :, 0:m, :], in0=zb[:, :, 0:m, :], in1=zb[:, :, m : 2 * m, :], op=ALU.add
            )

        def ca_of(c):
            if c not in ca_sb:
                ca_sb[c] = fin.tile([P, CH, H], F32, name="ca")
            return ca_sb[c]

        def on_pe(g):
            return g < PE_END and (g % PE_EVERY == PE_REST or g >= PE_TAIL)

        def sum_fill(g):
            t0, n = groups[g]
            ps = bank([P, n, P], F32)
            for i in range(n):
                for d in range(D):
                    nc.tensor.matmul(
                        ps[:, i, :],
                        lhsT=zb_sb[g][:, i, d, :],
                        rhs=ident_f[:],
                        start=(d == 0),
                        stop=(d == D - 1),
                        is_transpose=True,
                    )
            caT_ps[g] = ps

        def sum_evac(g):
            t0, n = groups[g]
            caT_sb[g] = t_pool.tile([P, n, P], F32, name="caT")
            nc.scalar.copy(out=caT_sb[g][:], in_=caT_ps[g][:])

        def sum_back(g):
            t0, n = groups[g]
            ps = bank([P, n, P], F32)
            for i in range(n):
                nc.tensor.transpose(ps[:, i, :], caT_sb[g][:, i, :], ident_f[:])
            ca_ps[g] = ps

        def sum_out(g):
            t0, n = groups[g]
            c, tt = divmod(t0, CH)
            nc.scalar.copy(out=ca_of(c)[:, tt : tt + n, :], in_=ca_ps[g][:])

        def add_last(g):
            t0, n = groups[g]
            c, tt = divmod(t0, CH)
            zb = zb_sb[g]
            ca_of(c)
            nc.vector.tensor_tensor(
                out=ca_sb[c][:, tt : tt + n, :], in0=zb[:, :, 0, :], in1=zb[:, :, 1, :], op=ALU.add
            )

        def mx(t):
            g = grp_of[t]
            codes, scales = code_sb[g]
            base = (t - groups[g][0]) * 256
            acc = bank([P, 3 * H], F32)
            for j0, j1 in COLS:
                for s in range(2):
                    nc.tensor.matmul_mx(
                        out=acc[:, j0:j1],
                        lhsT=codes[:, base + s * P : base + (s + 1) * P].bitcast(FP8X4),
                        lhsT_scale=scales[:, base + s * P : base + (s + 1) * P],
                        rhs=wcodes[:, s, j0:j1].bitcast(FP8X4),
                        rhs_scale=wscales[:, s, j0:j1],
                        start=(s == 0),
                        stop=(s == 1),
                    )
            acc_ps[t] = acc

        def st(t):
            c, tt = divmod(t, CH)
            if tt == 0:
                iou_sb[c] = fin.tile([P, CH, 3 * H], F32, name="iou_s")
            nc.vector.scalar_tensor_tensor(
                out=iou_sb[c][:, tt, :],
                in0=iou_all[:, t, :],
                scalar=2.0,
                in1=acc_ps[t][:],
                op0=ALU.mult,
                op1=ALU.add,
            )

        def w_fill(jb):
            wf = bank([P, D, P], BF16)
            for d in range(D):
                nc.tensor.transpose(wf[:, d, :], uis[:, jb, d * H : (d + 1) * H], ident_b[:])
            wf_ps[jb] = wf

        def w_evac(jb):
            nc.vector.tensor_copy(
                out=wg[:, :, jb * P : (jb + 1) * P, :],
                in_=wf_ps[jb][:].rearrange("p (s j) m -> p s m j", j=4),
            )

        def w_quant():
            for s in range(2):
                for j0, j1 in COLS:
                    nc.vector.quantize_mx(
                        out=wcodes[:, s, j0:j1].bitcast(FP8X4),
                        scales=wscales[:, s, j0:j1],
                        in_=wg[:, s, j0:j1, :].rearrange("p m j -> p (m j)"),
                    )

        def fa(e):
            t0, n = ends[e]
            c, tt = divmod(t0, CH)
            s = iou_sb[c][:, tt : tt + n, :]
            nc.scalar.activation(out=s[:, :, 0 : 2 * H], in_=s[:, :, 0 : 2 * H], func=ACT.Sigmoid)
            nc.scalar.activation(
                out=s[:, :, 2 * H : 3 * H], in_=s[:, :, 2 * H : 3 * H], func=ACT.Tanh
            )

        def f1(e):
            t0, n = ends[e]
            c, tt = divmod(t0, CH)
            s = iou_sb[c][:, tt : tt + n, :]
            if tt == 0:
                iu_sb[c] = fin.tile([P, CH, H], F32, name="iu")
            nc.vector.tensor_tensor(
                out=iu_sb[c][:, tt : tt + n, :], in0=s[:, :, 0:H], in1=s[:, :, 2 * H : 3 * H], op=ALU.mult
            )

        def f2(e):
            t0, n = ends[e]
            c, tt = divmod(t0, CH)
            if tt == 0:
                c_sb[c] = fin.tile([P, CH, H], F32, name="c_o")
            nc.vector.tensor_tensor(
                out=c_sb[c][:, tt : tt + n, :],
                in0=iu_sb[c][:, tt : tt + n, :],
                in1=ca_sb[c][:, tt : tt + n, :],
                op=ALU.add,
            )
            nc.sync.dma_start(out=c_out_v[:, t0 : t0 + n, :], in_=c_sb[c][:, tt : tt + n, :])

        def fb(e):
            t0, n = ends[e]
            c, tt = divmod(t0, CH)
            if tt == 0:
                tch_sb[c] = fin.tile([P, CH, H], F32, name="tch")
            nc.scalar.activation(
                out=tch_sb[c][:, tt : tt + n, :], in_=c_sb[c][:, tt : tt + n, :], func=ACT.Tanh
            )

        def f3(e):
            t0, n = ends[e]
            c, tt = divmod(t0, CH)
            if tt == 0:
                h_sb[c] = fin.tile([P, CH, H], F32, name="h_o")
            nc.vector.tensor_tensor(
                out=h_sb[c][:, tt : tt + n, :],
                in0=iou_sb[c][:, tt : tt + n, H : 2 * H],
                in1=tch_sb[c][:, tt : tt + n, :],
                op=ALU.mult,
            )
            nc.sync.dma_start(out=h_out_v[:, t0 : t0 + n, :], in_=h_sb[c][:, tt : tt + n, :])

        r_qx = [t0 + n - 1 + 2 for t0, n in groups]
        r_mu = [t0 + n - 1 + 4 for t0, n in groups]
        r_a1 = [r_mu[g + 1] if g + 1 < len(groups) else r_mu[g] + 1 for g in range(len(groups))]
        r_a2 = [x + 1 for x in r_a1]
        NEVER = -99
        r_sf = [r_mu[g] + 1 if on_pe(g) else NEVER for g in range(len(groups))]
        r_ca = [r_sf[g] + 3 if on_pe(g) else r_a2[g] for g in range(len(groups))]
        for g in range(len(groups)):
            if on_pe(g):
                r_a1[g] = NEVER
                r_a2[g] = NEVER
        r_mx = [max(r_qx[t | 1] + 1, W_READY + 1) for t in range(NT)]
        r_fa = [max(r_mx[t] for t in range(t0, t0 + n)) + 2 for t0, n in ends]
        r_f2 = [
            max(r_fa[e] + 1, max(r_ca[grp_of[t]] for t in range(ends[e][0], ends[e][0] + ends[e][1])) + 1)
            for e in range(len(ends))
        ]

        def due(rounds, r):
            return [i for i in range(len(rounds)) if rounds[i] == r]

        for r in range(0, max(r_f2) + 3):
            if r >= 5 and (r - 5) % CH == 0:
                m = (r - 5) // CH
                if m + 3 < NCH:
                    alloc_nh(m + 3)
                    load_nh(m + 3, 0, CH)
                if m + 2 < NCH:
                    alloc_c(m + 2)
                    load_c(m + 2, 0, CH)
            if ok(r - 3):
                sg(r - 3)
            for e in due(r_fa, r):
                fa(e)
            for e in due(r_f2, r - 1):
                fb(e)
            for g in due(r_sf, r - 1):
                sum_evac(g)
            for g in due(r_sf, r - 3):
                sum_out(g)
            if ok(r - 1):
                ex(r - 1)
            for g in range(NT // BG):
                if BG * g + 1 == r:
                    bt_evac(g)
            if r == W_READY - 1:
                for i in range(3):
                    w_evac(i)
            for g in due(r_a2, r):
                add_halves(g, 2)
            for g in due(r_mu, r):
                mu(g)
            for g in due(r_a2, r):
                add_last(g)
            for g in due(r_a1, r):
                add_halves(g, 4)
            for t in due(r_mx, r - 1):
                st(t)
            for g in due(r_qx, r):
                qx(g)
            if r == W_READY:
                w_quant()
            for e in due(r_fa, r - 1):
                f1(e)
            for e in due(r_f2, r - 2):
                f3(e)
            for e in due(r_f2, r):
                f2(e)
            if ok(r - 2):
                fm(r - 2)
            for t in due(r_mx, r):
                mx(t)
            for g in due(r_sf, r):
                sum_fill(g)
            for g in due(r_sf, r - 2):
                sum_back(g)
            if r == W_READY - 2:
                for i in range(3):
                    w_fill(i)
            if ok(r):
                tb(r)
            if r == 0:
                uf_fill()
            for g in range(NT // BG):
                if BG * g == r:
                    bt_fill(g)
